import numpy as np
import ml_dtypes


def mxq(x, axis, fmt="e4m3"):
    dtype, down = {"e4m3": (ml_dtypes.float8_e4m3fn, 7), "e5m2": (ml_dtypes.float8_e5m2, 14)}[fmt]
    v = np.moveaxis(np.asarray(x, np.float32).astype(ml_dtypes.bfloat16).astype(np.float64), axis, -1)
    blocks = v.reshape(v.shape[:-1] + (-1, 32))
    amax = np.abs(blocks).max(-1, keepdims=True)
    byte = np.maximum(np.where(amax > 0, np.frexp(amax)[1] - 1 + 127, 0) - down, 1)
    scale = np.exp2(byte - 127.0)
    codes = (blocks / scale).astype(np.float32).astype(dtype).astype(np.float64)
    return np.moveaxis((codes * scale).reshape(v.shape), -1, axis)


WIDE = False


def mx_kscale(k):
    if not WIDE:
        return np.ones(k)
    levels = np.array([30, -30])
    if k % 512:
        return np.exp2(np.random.permutation(np.resize(levels, k // 32))).repeat(32)
    a = np.empty((k // 512, 16))
    for p in range(k // 512):
        a[p, :8] = np.random.permutation(np.resize(levels, 8))
        for g in range(8):
            far = levels[np.abs(levels - a[p, g]) >= 10]
            a[p, g + 8] = far[np.random.randint(len(far))]
    return np.exp2(a.ravel()).repeat(32)


BF16 = ml_dtypes.bfloat16


def bf(x):
    return np.asarray(x, np.float32).astype(BF16)


def f64(x):
    return np.asarray(x).astype(np.float64)


T, B, I, H = 32, 128, 512, 512


def sigmoid(v):
    return 1.0 / (1.0 + np.exp(-v))


def setup_inputs():
    s = mx_kscale(I)
    return {
        "input": bf(np.random.standard_normal((T, B, I)) * s),
        "h0": bf(np.random.standard_normal((B, H))),
        "c0": bf(np.random.standard_normal((B, H))),
        "noise": bf(np.random.standard_normal((B, H)) * 0.3),
        "W_ih": bf(np.random.standard_normal((4 * H, I)) / np.sqrt(I) / s[None, :]),
        "W_hh": bf(np.random.standard_normal((4 * H, H)) * 0.7 / np.sqrt(H)),
        "b_ih": bf(np.random.standard_normal(4 * H) * 0.3),
        "b_hh": bf(np.random.standard_normal(4 * H) * 0.3),
    }


def reference(input, h0, c0, noise, W_ih, W_hh, b_ih, b_hh):
    hsz = h0.shape[-1]
    gx = mxq(f64(input), 2, "e5m2") @ mxq(f64(W_ih), 1, "e5m2").T
    gh = f64(h0) @ f64(W_hh).T
    gates = gx + gh[None, :, :] + (f64(b_ih) + f64(b_hh))
    i_g = sigmoid(gates[..., 0 * hsz:1 * hsz])
    f_g = sigmoid(gates[..., 1 * hsz:2 * hsz])
    g_g = np.tanh(gates[..., 2 * hsz:3 * hsz])
    o_g = sigmoid(gates[..., 3 * hsz:4 * hsz])
    c = f_g * f64(c0)[None] + i_g * g_g
    h = o_g * np.tanh(c) + f64(noise)[None]
    return (h, np.stack([h[-1], c[-1]]))

@@ -1,0 +1,325 @@
+from contextlib import ExitStack
+
+import concourse.mybir as mybir
+from concourse.masks import make_identity
+
+T, B, I, H = 32, 128, 512, 512
+FLOPS = 2 * T * B * I * 4 * H + 2 * B * H * 4 * H
+
+F32 = mybir.dt.float32
+BF16 = mybir.dt.bfloat16
+U32 = mybir.dt.uint32
+U8 = mybir.dt.uint8
+E5M2X4 = mybir.dt.float8_e5m2_x4
+ACT = mybir.ActivationFunctionType
+ALU = mybir.AluOpType
+
+P = 128
+STEPS = 4
+GROUPS = T // STEPS
+CHUNKS = H // P
+UNITS = GROUPS * CHUNKS
+GATE_I, GATE_F, GATE_G, GATE_O = 0, 1, 2, 3
+GATE_ORDER = (GATE_F, GATE_I, GATE_G, GATE_O)
+
+
+def tile_lstmlayer_kernel(tc, x, h0, c0, noise, w_ih, w_hh, b_ih, b_hh, out_h, out_state):
+    nc = tc.nc
+    order = [(0, 0), (0, 1), (1, 0), (1, 1)] + [(j, g) for g in range(2, GROUPS) for j in (0, 1)]
+    order += [(j, g) for j in (2, 3) for g in range(GROUPS)]
+    with ExitStack() as ctx:
+        keep = ctx.enter_context(tc.tile_pool(name="keep", bufs=1))
+        work = ctx.enter_context(tc.tile_pool(name="work", bufs=3))
+        psum = ctx.enter_context(tc.psum_pool(name="psum", bufs=1))
+        ctx.enter_context(tc.manual_schedule())
+
+        ident_f = keep.tile([P, P], F32, name="ident_f")
+        ident_b = keep.tile([P, P], BF16, name="ident_b")
+        ones_b = keep.tile([P, P], BF16, name="ones_b")
+        bias_rows = keep.tile([P, 4 * H], BF16, name="bias_rows")
+        nc.vector.memset(bias_rows[:], 0.0)
+        make_identity(nc, ident_b[:])
+        make_identity(nc, ident_f[:])
+        nc.vector.memset(ones_b[:], 1.0)
+
+        x_sb = [keep.tile([P, STEPS, I], BF16, name="x_sb%d" % g) for g in range(GROUPS)]
+        wih_sb = [keep.tile([P, 4, I], BF16, name="wih_sb%d" % j) for j in range(CHUNKS)]
+        whh_sb = [keep.tile([P, 4, H], BF16, name="whh_sb%d" % j) for j in range(CHUNKS)]
+        h0_sb = keep.tile([P, H], BF16, name="h0_sb")
+        c0_sb = keep.tile([P, H], BF16, name="c0_sb")
+        noise_sb = keep.tile([P, H], BF16, name="noise_sb")
+        wih_v = w_ih.rearrange("(g j p) k -> j p g k", g=4, j=CHUNKS)
+        whh_v = w_hh.rearrange("(g j p) k -> j p g k", g=4, j=CHUNKS)
+
+        def load_x(g):
+            nc.sync.dma_start(out=x_sb[g][:], in_=x[g * STEPS:(g + 1) * STEPS].rearrange("t b k -> b t k"))
+
+        nc.sync.dma_start(out=h0_sb[:], in_=h0)
+        nc.sync.dma_start(out=whh_sb[0][:, 0:2], in_=whh_v[0][:, 0:2])
+        x0_v = x[0:STEPS].rearrange("t b k -> b t k")
+        nc.sync.dma_start(out=x_sb[0][:, 0:2], in_=x0_v[:, 0:2])
+        nc.scalar.dma_start(out=bias_rows[0:1, :], in_=b_ih.rearrange("(o n) -> o n", o=1))
+        nc.scalar.dma_start(out=bias_rows[1:2, :], in_=b_hh.rearrange("(o n) -> o n", o=1))
+        nc.sync.dma_start(out=x_sb[0][:, 2:4], in_=x0_v[:, 2:4])
+        nc.sync.dma_start(out=wih_sb[0][:, 0:2], in_=wih_v[0][:, 0:2])
+        nc.sync.dma_start(out=wih_sb[0][:, 2:4], in_=wih_v[0][:, 2:4])
+        nc.sync.dma_start(out=whh_sb[0][:, 2:4], in_=whh_v[0][:, 2:4])
+        x1_v = x[STEPS:2 * STEPS].rearrange("t b k -> b t k")
+        nc.sync.dma_start(out=x_sb[1][:, 0:2], in_=x1_v[:, 0:2])
+        nc.sync.dma_start(out=x_sb[1][:, 2:4], in_=x1_v[:, 2:4])
+        nc.sync.dma_start(out=c0_sb[:], in_=c0)
+        nc.sync.dma_start(out=wih_sb[1][:], in_=wih_v[1])
+        nc.sync.dma_start(out=whh_sb[1][:], in_=whh_v[1])
+        nc.sync.dma_start(out=noise_sb[:], in_=noise)
+        load_x(2)
+        load_x(3)
+        nc.sync.dma_start(out=whh_sb[2][:], in_=whh_v[2])
+        for g in range(4, GROUPS):
+            load_x(g)
+        nc.sync.dma_start(out=wih_sb[2][:], in_=wih_v[2])
+        nc.sync.dma_start(out=whh_sb[3][:], in_=whh_v[3])
+        nc.sync.dma_start(out=wih_sb[3][:], in_=wih_v[3])
+
+        x_codes = [keep.tile([P, STEPS * P], U32, name="x_codes%d" % g, align_bytes=64) for g in range(GROUPS)]
+        x_scales = [keep.tile([P, STEPS * P], U8, name="x_scales%d" % g, align_bytes=64) for g in range(GROUPS)]
+        w_codes = [keep.tile([P, 4 * P], U32, name="w_codes%d" % j, align_bytes=64) for j in range(CHUNKS)]
+        w_scales = [keep.tile([P, 4 * P], U8, name="w_scales%d" % j, align_bytes=64) for j in range(CHUNKS)]
+        grouped_tiles = {}
+
+        def grouped_for(key):
+            if key not in grouped_tiles:
+                grouped_tiles[key] = work.tile([P, 4 * I], BF16, name="grouped", align_bytes=64)
+            return grouped_tiles[key]
+
+        whh_t = [keep.tile([P, 4, CHUNKS, P], BF16, name="whh_t%d" % j) for j in range(CHUNKS)]
+        base = [keep.tile([P, 4, P], F32, name="base%d" % j) for j in range(CHUNKS)]
+        h0_t = keep.tile([P, CHUNKS, P], BF16, name="h0_t")
+        c_last = keep.tile([P, H], F32, name="c_last")
+
+        def copy_on(engine, out, in_):
+            if engine == "vector":
+                nc.vector.tensor_copy(out=out, in_=in_)
+            else:
+                nc.scalar.copy(out=out, in_=in_)
+
+        def turn_words(src, grouped, half, tag="prep", bufs=2):
+            words = src[:].rearrange("p q k -> p (q k)").bitcast(F32)
+            bank = psum.tile([P, 2, 2, P], F32, name="bank_words", tag=tag, bufs=bufs)
+            for r in range(2):
+                w0 = (2 * half + r) * (I // 2)
+                for u in range(2):
+                    nc.tensor.transpose(bank[:, r, u, :], words[:, w0 + u:w0 + I // 2:2], ident_f[:])
+            dst = grouped[:].bitcast(F32).rearrange("p (q c u) -> p q c u", q=4, u=2)[:, 2 * half:2 * half + 2]
+            return lambda engine: copy_on(engine, dst, bank[:].rearrange("p r u c -> p r c u"))
+
+        def turn_whh(j, half, tag="prep", bufs=2):
+            bank = psum.tile([P, 2, CHUNKS, P], BF16, name="bank_whh", tag=tag, bufs=bufs)
+            for r in range(2):
+                for kc in range(CHUNKS):
+                    nc.tensor.transpose(bank[:, r, kc, :], whh_sb[j][:, 2 * half + r, kc * P:(kc + 1) * P], ident_b[:])
+            return lambda engine: copy_on(engine, whh_t[j][:, 2 * half:2 * half + 2], bank[:])
+
+        def base_gates(j, half, tag="prep", bufs=2):
+            bank = psum.tile([P, 2, P], F32, name="bank_base", tag=tag, bufs=bufs)
+            for r in range(2):
+                gate = 2 * half + r
+                bias = bias_rows[:, gate * H + j * P:gate * H + (j + 1) * P]
+                pairs = [(whh_t[j][:, gate, kc, :], h0_t[:, kc, :]) for kc in range(CHUNKS)] + [(bias, ones_b[:])]
+                for n, (by_channel, by_row) in enumerate(pairs):
+                    lhsT, rhs = (by_row, by_channel) if gate == GATE_O else (by_channel, by_row)
+                    nc.tensor.matmul(bank[:, r, :], lhsT=lhsT, rhs=rhs, start=(n == 0), stop=(n == len(pairs) - 1))
+            return lambda engine: copy_on(engine, base[j][:, 2 * half:2 * half + 2], bank[:])
+
+        def quantize(grouped, codes, scales, lo=0, hi=4):
+            nc.vector.quantize_mx(out=codes[:, lo * P:hi * P].bitcast(E5M2X4), scales=scales[:, lo * P:hi * P], in_=grouped[:, lo * I:hi * I])
+
+        gate_bank, pre, act, prod_f, prod_i, c_bank, tanh_c, h_raw = {}, {}, {}, {}, {}, {}, {}, {}
+
+        def project(s, gates=GATE_ORDER):
+            j, g = order[s]
+            for gate in gates:
+                bank = psum.tile([P, STEPS, P], F32, name="bank_gate", tag="gate%d" % gate, bufs=1)
+                cols = slice(gate * P, (gate + 1) * P)
+                if gate == GATE_O:
+                    for t in range(STEPS):
+                        rows = slice(t * P, (t + 1) * P)
+                        nc.tensor.matmul_mx(
+                            out=bank[:, t, :],
+                            lhsT=x_codes[g][:, rows].bitcast(E5M2X4), lhsT_scale=x_scales[g][:, rows],
+                            rhs=w_codes[j][:, cols].bitcast(E5M2X4), rhs_scale=w_scales[j][:, cols],
+                            start=True, stop=True)
+                else:
+                    nc.tensor.matmul_mx(
+                        out=bank[:].rearrange("p t b -> p (t b)"),
+                        lhsT=w_codes[j][:, cols].bitcast(E5M2X4), lhsT_scale=w_scales[j][:, cols],
+                        rhs=x_codes[g][:].bitcast(E5M2X4), rhs_scale=x_scales[g][:],
+                        start=True, stop=True)
+                gate_bank[s, gate] = bank
+
+        def over_steps(ap):
+            return ap.unsqueeze(1).to_broadcast([P, STEPS, P])
+
+        def add_base(s, gate):
+            j = order[s][0]
+            pre[s, gate] = work.tile([P, STEPS, P], F32, name="pre", tag="pre%d" % gate, bufs=2)
+            nc.vector.tensor_tensor(out=pre[s, gate][:], in0=over_steps(base[j][:, gate, :]),
+                                    in1=gate_bank[s, gate][:], op=ALU.add)
+
+        def activate(s, gate):
+            act[s, gate] = work.tile([P, STEPS, P], F32, name="act", tag="act%d" % gate, bufs=5 if gate == GATE_O else 3)
+            nc.scalar.activation(out=act[s, gate][:], in_=pre[s, gate][:],
+                                 func=ACT.Tanh if gate == GATE_G else ACT.Sigmoid)
+
+        def forget(s):
+            j = order[s][0]
+            prod_f[s] = work.tile([P, STEPS, P], F32, name="prod_f")
+            nc.vector.tensor_tensor(out=prod_f[s][:], in0=act[s, GATE_F][:], in1=over_steps(consts[:, 0, j, :]), op=ALU.mult)
+
+        def admit(s, engine):
+            prod_i[s] = work.tile([P, STEPS, P], F32, name="prod_i")
+            engine.tensor_tensor(out=prod_i[s][:], in0=act[s, GATE_I][:], in1=act[s, GATE_G][:], op=ALU.mult)
+
+        def sum_cell(s, tag="cell"):
+            c_bank[s] = psum.tile([P, STEPS, P], F32, name="bank_c", tag=tag, bufs=1)
+            for t in range(STEPS):
+                nc.tensor.matmul(c_bank[s][:, t, :], lhsT=prod_f[s][:, t, :], rhs=ident_f[:], is_transpose=True, start=True, stop=False)
+                nc.tensor.matmul(c_bank[s][:, t, :], lhsT=prod_i[s][:, t, :], rhs=ident_f[:], is_transpose=True, start=False, stop=True)
+
+        def squash_cell(s):
+            j, g = order[s]
+            tanh_c[s] = work.tile([P, STEPS, P], F32, name="tanh_c")
+            nc.scalar.activation(out=tanh_c[s][:], in_=c_bank[s][:], func=ACT.Tanh)
+            if g == GROUPS - 1:
+                nc.scalar.copy(out=c_last[:, j * P:(j + 1) * P], in_=c_bank[s][:, STEPS - 1, :])
+                nc.sync.dma_start(out=out_state[1, :, j * P:(j + 1) * P], in_=c_last[:, j * P:(j + 1) * P])
+
+        def emit(s, engine):
+            h_raw[s] = work.tile([P, STEPS, P], F32, name="h_raw")
+            engine.tensor_tensor(out=h_raw[s][:], in0=act[s, GATE_O][:], in1=tanh_c[s][:], op=ALU.mult)
+
+        def add_noise_and_store(s, on_vector):
+            j, g = order[s]
+            cols = slice(j * P, (j + 1) * P)
+            h_out = work.tile([P, STEPS, P], F32, name="h_out", bufs=6)
+            if on_vector:
+                nc.vector.tensor_tensor(out=h_out[:], in0=h_raw[s][:], in1=over_steps(consts[:, 1, j, :]), op=ALU.add)
+            else:
+                nc.gpsimd.tensor_tensor(out=h_out[:], in0=h_raw[s][:], in1=over_steps(noise_sb[:, cols]), op=ALU.add)
+            nc.sync.dma_start(out=out_h[g * STEPS:(g + 1) * STEPS, :, cols].rearrange("t b c -> b t c"), in_=h_out[:])
+            if g == GROUPS - 1:
+                nc.sync.dma_start(out=out_state[0, :, cols], in_=h_out[:, STEPS - 1, :])
+
+        bank_h0 = psum.tile([P, CHUNKS, P], BF16, name="bank_h0", tag="cell", bufs=1)
+        for kc in range(CHUNKS):
+            nc.tensor.transpose(bank_h0[:, kc, :], h0_sb[:, kc * P:(kc + 1) * P], ident_b[:])
+        nc.scalar.copy(out=h0_t[:], in_=bank_h0[:])
+        turn_whh(0, 0, "gate2", 1)("vector")
+        turn_words(x_sb[0], grouped_for(("x", 0)), 0)("scalar")
+        turn_words(x_sb[0], grouped_for(("x", 0)), 1)("vector")
+        turn_words(wih_sb[0], grouped_for(("w", 0)), 0, "gate3", 1)("scalar")
+        copy_base = base_gates(0, 0, "cell", 1)
+        quantize(grouped_for(("x", 0)), x_codes[0], x_scales[0])
+        copy_base("scalar")
+        quantize(grouped_for(("w", 0)), w_codes[0], w_scales[0], 0, 2)
+        turn_words(wih_sb[0], grouped_for(("w", 0)), 1)("scalar")
+        turn_whh(0, 1)("scalar")
+        project(0, (GATE_F, GATE_I))
+        quantize(grouped_for(("w", 0)), w_codes[0], w_scales[0], 2, 4)
+        copy_a = turn_words(x_sb[1], grouped_for(("x", 1)), 0)
+        copy_base = base_gates(0, 1, "cell", 1)
+        project(0, (GATE_G, GATE_O))
+        copy_b = turn_words(x_sb[1], grouped_for(("x", 1)), 1)
+        add_base(0, GATE_F)
+        activate(0, GATE_F)
+        add_base(0, GATE_I)
+        activate(0, GATE_I)
+        copy_a("vector")
+        copy_base("vector")
+        consts = psum.tile([P, 2, CHUNKS, P], BF16, name="consts", tag="consts", bufs=1)
+        for j in range(CHUNKS):
+            nc.tensor.transpose(consts[:, 0, j, :], c0_sb[:, j * P:(j + 1) * P], ident_b[:])
+        add_base(0, GATE_G)
+        activate(0, GATE_G)
+        copy_b("vector")
+        add_base(0, GATE_O)
+        copy_a = turn_words(wih_sb[1], grouped_for(("w", 1)), 0)
+        copy_c = turn_whh(1, 0, "cell", 1)
+        quantize(grouped_for(("x", 1)), x_codes[1], x_scales[1])
+        project(1, (GATE_F, GATE_I))
+        copy_b = turn_words(wih_sb[1], grouped_for(("w", 1)), 1)
+        project(1, (GATE_G, GATE_O))
+        copy_a("scalar")
+        forget(0)
+        activate(0, GATE_O)
+        copy_b("scalar")
+        copy_c("vector")
+        nc.tensor.matmul(consts[:, 1].rearrange("p j c -> p (j c)"), lhsT=ident_b[:], rhs=noise_sb[:], start=True, stop=True)
+
+        jobs = {s: [] for s in range(UNITS + 4)}
+        quants = {1: ("w", 1), 15: ("w", 2), 23: ("w", 3)}
+        jobs[1] += [lambda: turn_whh(1, 1), lambda: base_gates(1, 0)]
+        jobs[2] += [lambda: base_gates(1, 1)]
+        for g in range(2, GROUPS):
+            for half in range(2):
+                jobs[max(2 * g - 3 + half, 2)].append(lambda g=g, half=half: turn_words(x_sb[g], grouped_for(("x", g)), half))
+            quants[2 * g - 1] = ("x", g)
+        for j, ticks in ((2, (5, 7, 9, 11, 13, 14)), (3, (16, 17, 18, 19, 21, 22))):
+            for half in range(2):
+                jobs[ticks[half]].append(lambda j=j, half=half: turn_whh(j, half))
+                jobs[ticks[2 + half]].append(lambda j=j, half=half: base_gates(j, half))
+                jobs[ticks[4 + half]].append(lambda j=j, half=half: turn_words(wih_sb[j], grouped_for(("w", j)), half))
+        for s in range(1, UNITS):
+            live = s < UNITS
+            copies = [job() for job in jobs[s][:2]]
+            noise_on_vector = s % 2 == 0 or s == UNITS - 1
+            if s <= UNITS:
+                admit(s - 1, nc.gpsimd)
+            if 3 <= s <= UNITS + 2:
+                emit(s - 3, nc.gpsimd)
+            if s >= 4 and not noise_on_vector:
+                add_noise_and_store(s - 4, False)
+            if live:
+                add_base(s, GATE_F)
+                activate(s, GATE_F)
+                if s <= 2:
+                    for copy in copies[:1]:
+                        copy("scalar")
+                add_base(s, GATE_I)
+                activate(s, GATE_I)
+                if s in quants:
+                    kind, n = quants[s]
+                    quantize(grouped_for(quants[s]), (x_codes if kind == "x" else w_codes)[n], (x_scales if kind == "x" else w_scales)[n])
+                if s <= 2:
+                    for copy in copies[1:]:
+                        copy("vector")
+                    for job in jobs[s][2:]:
+                        job()("scalar")
+            if 2 <= s <= UNITS + 1:
+                squash_cell(s - 2)
+            if live:
+                add_base(s, GATE_G)
+                activate(s, GATE_G)
+                if s > 2:
+                    for copy in copies:
+                        copy("scalar")
+                add_base(s, GATE_O)
+                activate(s, GATE_O)
+                if s + 1 < UNITS:
+                    project(s + 1)
+                forget(s)
+            if s >= 4 and noise_on_vector:
+                add_noise_and_store(s - 4, True)
+            if s <= UNITS:
+                sum_cell(s - 1)
+        last = UNITS - 1
+        emit(last - 2, nc.gpsimd)
+        add_noise_and_store(last - 3, True)
+        admit(last, nc.vector)
+        squash_cell(last - 1)
+        sum_cell(last, "gate1")
+        add_noise_and_store(last - 2, True)
+        emit(last - 1, nc.vector)
+        squash_cell(last)
+        add_noise_and_store(last - 1, True)
+        emit(last, nc.vector)
+        add_noise_and_store(last, True)

@@ -116,7 +116,7 @@ def tile_lstmlayer_kernel(tc, x, h0, c0, noise, w_ih, w_hh, b_ih, b_hh, out_h, o
             bank = psum.tile([P, 2, CHUNKS, P], BF16, name="bank_whh", tag=tag, bufs=bufs)
             for r in range(2):
                 for kc in range(CHUNKS):
-                    nc.tensor.transpose(bank[:, r, kc, :], whh_sb[j][:, 2 * half + r, kc * P:(kc + 1) * P], ident_b[:])
+                    nc.tensor.matmul(bank[:, r, kc, :], lhsT=whh_sb[j][:, 2 * half + r, kc * P:(kc + 1) * P], rhs=ident_b[:], start=True, stop=True)
             return lambda engine: copy_on(engine, whh_t[j][:, 2 * half:2 * half + 2], bank[:])
 
         def base_gates(j, half, tag="prep", bufs=2):
@@ -211,114 +211,134 @@ def tile_lstmlayer_kernel(tc, x, h0, c0, noise, w_ih, w_hh, b_ih, b_hh, out_h, o
 
         bank_h0 = psum.tile([P, CHUNKS, P], BF16, name="bank_h0", tag="cell", bufs=1)
         for kc in range(CHUNKS):
-            nc.tensor.transpose(bank_h0[:, kc, :], h0_sb[:, kc * P:(kc + 1) * P], ident_b[:])
+            nc.tensor.matmul(bank_h0[:, kc, :], lhsT=h0_sb[:, kc * P:(kc + 1) * P], rhs=ident_b[:], start=True, stop=True)
         nc.scalar.copy(out=h0_t[:], in_=bank_h0[:])
         turn_whh(0, 0, "gate2", 1)("vector")
         turn_words(x_sb[0], grouped_for(("x", 0)), 0)("scalar")
         turn_words(x_sb[0], grouped_for(("x", 0)), 1)("vector")
+        base_gates(0, 0, "cell", 1)("scalar")
         turn_words(wih_sb[0], grouped_for(("w", 0)), 0, "gate3", 1)("scalar")
-        copy_base = base_gates(0, 0, "cell", 1)
         quantize(grouped_for(("x", 0)), x_codes[0], x_scales[0])
-        copy_base("scalar")
-        quantize(grouped_for(("w", 0)), w_codes[0], w_scales[0], 0, 2)
+        turn_whh(0, 1, "gate2", 1)("vector")
         turn_words(wih_sb[0], grouped_for(("w", 0)), 1)("scalar")
-        turn_whh(0, 1)("scalar")
+        quantize(grouped_for(("w", 0)), w_codes[0], w_scales[0], 0, 2)
+        base_gates(0, 1, "cell", 1)("scalar")
         project(0, (GATE_F, GATE_I))
         quantize(grouped_for(("w", 0)), w_codes[0], w_scales[0], 2, 4)
-        copy_a = turn_words(x_sb[1], grouped_for(("x", 1)), 0)
-        copy_base = base_gates(0, 1, "cell", 1)
+        turn_words(x_sb[1], grouped_for(("x", 1)), 0)("scalar")
         project(0, (GATE_G, GATE_O))
-        copy_b = turn_words(x_sb[1], grouped_for(("x", 1)), 1)
+        copy_x = turn_words(x_sb[1], grouped_for(("x", 1)), 1)
         add_base(0, GATE_F)
         activate(0, GATE_F)
         add_base(0, GATE_I)
         activate(0, GATE_I)
-        copy_a("vector")
-        copy_base("vector")
+        add_base(0, GATE_G)
+        copy_x("vector")
+        activate(0, GATE_G)
+        copy_h = turn_whh(1, 0, "cell", 1)
+        copy_w = turn_words(wih_sb[1], grouped_for(("w", 1)), 0)
         consts = psum.tile([P, 2, CHUNKS, P], BF16, name="consts", tag="consts", bufs=1)
         for j in range(CHUNKS):
-            nc.tensor.transpose(consts[:, 0, j, :], c0_sb[:, j * P:(j + 1) * P], ident_b[:])
-        add_base(0, GATE_G)
-        activate(0, GATE_G)
-        copy_b("vector")
-        add_base(0, GATE_O)
-        copy_a = turn_words(wih_sb[1], grouped_for(("w", 1)), 0)
-        copy_c = turn_whh(1, 0, "cell", 1)
-        quantize(grouped_for(("x", 1)), x_codes[1], x_scales[1])
-        project(1, (GATE_F, GATE_I))
-        copy_b = turn_words(wih_sb[1], grouped_for(("w", 1)), 1)
-        project(1, (GATE_G, GATE_O))
-        copy_a("scalar")
-        forget(0)
-        activate(0, GATE_O)
-        copy_b("scalar")
-        copy_c("vector")
+            nc.tensor.matmul(consts[:, 0, j, :], lhsT=c0_sb[:, j * P:(j + 1) * P], rhs=ident_b[:], start=True, stop=True)
         nc.tensor.matmul(consts[:, 1].rearrange("p j c -> p (j c)"), lhsT=ident_b[:], rhs=noise_sb[:], start=True, stop=True)
-
-        jobs = {s: [] for s in range(UNITS + 4)}
-        quants = {1: ("w", 1), 15: ("w", 2), 23: ("w", 3)}
-        jobs[1] += [lambda: turn_whh(1, 1), lambda: base_gates(1, 0)]
-        jobs[2] += [lambda: base_gates(1, 1)]
-        for g in range(2, GROUPS):
-            for half in range(2):
-                jobs[max(2 * g - 3 + half, 2)].append(lambda g=g, half=half: turn_words(x_sb[g], grouped_for(("x", g)), half))
-            quants[2 * g - 1] = ("x", g)
-        for j, ticks in ((2, (5, 7, 9, 11, 13, 14)), (3, (16, 17, 18, 19, 21, 22))):
+        add_base(0, GATE_O)
+        quantize(grouped_for(("x", 1)), x_codes[1], x_scales[1])
+        copy_h("vector")
+        copy_w("scalar")
+        copy_w = turn_words(wih_sb[1], grouped_for(("w", 1)), 1)
+        admit(0, nc.gpsimd)
+        project(1, (GATE_F, GATE_I))
+        copy_h = turn_whh(1, 1)
+        project(1, (GATE_G, GATE_O))
+        copy_w("scalar")
+        activate(0, GATE_O)
+        forget(0)
+        add_base(1, GATE_F)
+        copy_h("scalar")
+        activate(1, GATE_F)
+        quantize(grouped_for(("w", 1)), w_codes[1], w_scales[1])
+        copy_b = base_gates(1, 0)
+        sum_cell(0)
+        add_base(1, GATE_I)
+        activate(1, GATE_I)
+        copy_b("vector")
+        copy_b = base_gates(1, 1)
+        project(2, (GATE_F, GATE_I))
+        add_base(1, GATE_G)
+        activate(1, GATE_G)
+        add_base(1, GATE_O)
+        copy_x = turn_words(x_sb[2], grouped_for(("x", 2)), 0)
+        project(2, (GATE_G, GATE_O))
+        copy_b("vector")
+        activate(1, GATE_O)
+        admit(1, nc.gpsimd)
+        squash_cell(0)
+        emit(0, nc.gpsimd)
+        add_base(2, GATE_F)
+        copy_x("scalar")
+        copy_x = turn_words(x_sb[2], grouped_for(("x", 2)), 1)
+        activate(2, GATE_F)
+        add_base(2, GATE_I)
+        activate(2, GATE_I)
+        project(3, (GATE_F, GATE_I))
+        forget(1)
+        sum_cell(1)
+        add_base(2, GATE_G)
+        copy_x("scalar")
+        activate(2, GATE_G)
+        add_base(2, GATE_O)
+        activate(2, GATE_O)
+        project(3, (GATE_G, GATE_O))
+        quantize(grouped_for(("x", 2)), x_codes[2], x_scales[2])
+        copies = [turn_words(x_sb[3], grouped_for(("x", 3)), 0)]
+        jobs = {s: [] for s in range(UNITS)}
+        quants = {14: ("w", 2), 22: ("w", 3)}
+        for g in range(3, GROUPS):
+            for half in range(1 if g == 3 else 0, 2):
+                jobs[max(2 * g - 4 + half, 3)].append(lambda g=g, half=half: turn_words(x_sb[g], grouped_for(("x", g)), half))
+            quants[2 * g - 2] = ("x", g)
+        for j, ticks in ((2, (4, 6, 8, 10, 11, 12)), (3, (15, 16, 17, 18, 19, 20))):
             for half in range(2):
                 jobs[ticks[half]].append(lambda j=j, half=half: turn_whh(j, half))
                 jobs[ticks[2 + half]].append(lambda j=j, half=half: base_gates(j, half))
                 jobs[ticks[4 + half]].append(lambda j=j, half=half: turn_words(wih_sb[j], grouped_for(("w", j)), half))
-        for s in range(1, UNITS):
-            live = s < UNITS
-            copies = [job() for job in jobs[s][:2]]
-            noise_on_vector = s % 2 == 0 or s == UNITS - 1
-            if s <= UNITS:
-                admit(s - 1, nc.gpsimd)
-            if 3 <= s <= UNITS + 2:
-                emit(s - 3, nc.gpsimd)
-            if s >= 4 and not noise_on_vector:
-                add_noise_and_store(s - 4, False)
-            if live:
-                add_base(s, GATE_F)
-                activate(s, GATE_F)
-                if s <= 2:
-                    for copy in copies[:1]:
-                        copy("scalar")
-                add_base(s, GATE_I)
-                activate(s, GATE_I)
-                if s in quants:
-                    kind, n = quants[s]
-                    quantize(grouped_for(quants[s]), (x_codes if kind == "x" else w_codes)[n], (x_scales if kind == "x" else w_scales)[n])
-                if s <= 2:
-                    for copy in copies[1:]:
-                        copy("vector")
-                    for job in jobs[s][2:]:
-                        job()("scalar")
-            if 2 <= s <= UNITS + 1:
+        for s in range(3, UNITS):
+            noise_on_vector = s % 2 == 0
+            admit(s - 1, nc.gpsimd)
+            if s >= 2:
                 squash_cell(s - 2)
-            if live:
-                add_base(s, GATE_G)
-                activate(s, GATE_G)
-                if s > 2:
-                    for copy in copies:
-                        copy("scalar")
-                add_base(s, GATE_O)
-                activate(s, GATE_O)
-                if s + 1 < UNITS:
-                    project(s + 1)
-                forget(s)
-            if s >= 4 and noise_on_vector:
-                add_noise_and_store(s - 4, True)
-            if s <= UNITS:
-                sum_cell(s - 1)
+                emit(s - 2, nc.gpsimd)
+            if s >= 3 and not noise_on_vector:
+                add_noise_and_store(s - 3, False)
+            add_base(s, GATE_F)
+            activate(s, GATE_F)
+            add_base(s, GATE_I)
+            activate(s, GATE_I)
+            if s + 1 < UNITS:
+                project(s + 1, (GATE_F, GATE_I))
+            for copy in copies:
+                copy("scalar")
+            forget(s - 1)
+            sum_cell(s - 1)
+            add_base(s, GATE_G)
+            activate(s, GATE_G)
+            add_base(s, GATE_O)
+            activate(s, GATE_O)
+            if s + 1 < UNITS:
+                project(s + 1, (GATE_G, GATE_O))
+            if s >= 3 and noise_on_vector:
+                add_noise_and_store(s - 3, True)
+            if s in quants:
+                kind, n = quants[s]
+                quantize(grouped_for(quants[s]), (x_codes if kind == "x" else w_codes)[n], (x_scales if kind == "x" else w_scales)[n])
+            copies = [job() for job in jobs[s]]
         last = UNITS - 1
-        emit(last - 2, nc.gpsimd)
-        add_noise_and_store(last - 3, True)
+        forget(last)
         admit(last, nc.vector)
         squash_cell(last - 1)
         sum_cell(last, "gate1")
+        emit(last - 1, nc.gpsimd)
         add_noise_and_store(last - 2, True)
-        emit(last - 1, nc.vector)
         squash_cell(last)
         add_noise_and_store(last - 1, True)
         emit(last, nc.vector)

@@ -20,12 +20,13 @@ GROUPS = T // STEPS
 CHUNKS = H // P
 UNITS = GROUPS * CHUNKS
 GATE_I, GATE_F, GATE_G, GATE_O = 0, 1, 2, 3
+LAG = 3
 GATE_ORDER = (GATE_F, GATE_I, GATE_G, GATE_O)
 
 
 def tile_lstmlayer_kernel(tc, x, h0, c0, noise, w_ih, w_hh, b_ih, b_hh, out_h, out_state):
     nc = tc.nc
-    order = [(0, 0), (0, 1), (1, 0), (1, 1)] + [(j, g) for g in range(2, GROUPS) for j in (0, 1)]
+    order = [(j, g) for j in (0, 1) for g in range(3)] + [(j, g) for g in range(3, GROUPS) for j in (0, 1)]
     order += [(j, g) for j in (2, 3) for g in range(GROUPS)]
     with ExitStack() as ctx:
         keep = ctx.enter_context(tc.tile_pool(name="keep", bufs=1))
@@ -54,24 +55,24 @@ def tile_lstmlayer_kernel(tc, x, h0, c0, noise, w_ih, w_hh, b_ih, b_hh, out_h, o
         def load_x(g):
             nc.sync.dma_start(out=x_sb[g][:], in_=x[g * STEPS:(g + 1) * STEPS].rearrange("t b k -> b t k"))
 
+        x0_v = x[0:STEPS].rearrange("t b k -> b t k")
+        x1_v = x[STEPS:2 * STEPS].rearrange("t b k -> b t k")
+        nc.sync.dma_start(out=x_sb[0][:, 0:2], in_=x0_v[:, 0:2])
         nc.sync.dma_start(out=h0_sb[:], in_=h0)
         nc.sync.dma_start(out=whh_sb[0][:, 0:2], in_=whh_v[0][:, 0:2])
-        x0_v = x[0:STEPS].rearrange("t b k -> b t k")
-        nc.sync.dma_start(out=x_sb[0][:, 0:2], in_=x0_v[:, 0:2])
         nc.scalar.dma_start(out=bias_rows[0:1, :], in_=b_ih.rearrange("(o n) -> o n", o=1))
         nc.scalar.dma_start(out=bias_rows[1:2, :], in_=b_hh.rearrange("(o n) -> o n", o=1))
         nc.sync.dma_start(out=x_sb[0][:, 2:4], in_=x0_v[:, 2:4])
         nc.sync.dma_start(out=wih_sb[0][:, 0:2], in_=wih_v[0][:, 0:2])
-        nc.sync.dma_start(out=wih_sb[0][:, 2:4], in_=wih_v[0][:, 2:4])
         nc.sync.dma_start(out=whh_sb[0][:, 2:4], in_=whh_v[0][:, 2:4])
-        x1_v = x[STEPS:2 * STEPS].rearrange("t b k -> b t k")
+        nc.sync.dma_start(out=wih_sb[0][:, 2:4], in_=wih_v[0][:, 2:4])
+        nc.sync.dma_start(out=c0_sb[:], in_=c0)
+        nc.sync.dma_start(out=noise_sb[:], in_=noise)
         nc.sync.dma_start(out=x_sb[1][:, 0:2], in_=x1_v[:, 0:2])
         nc.sync.dma_start(out=x_sb[1][:, 2:4], in_=x1_v[:, 2:4])
-        nc.sync.dma_start(out=c0_sb[:], in_=c0)
-        nc.sync.dma_start(out=wih_sb[1][:], in_=wih_v[1])
-        nc.sync.dma_start(out=whh_sb[1][:], in_=whh_v[1])
-        nc.sync.dma_start(out=noise_sb[:], in_=noise)
         load_x(2)
+        nc.sync.dma_start(out=whh_sb[1][:], in_=whh_v[1])
+        nc.sync.dma_start(out=wih_sb[1][:], in_=wih_v[1])
         load_x(3)
         nc.sync.dma_start(out=whh_sb[2][:], in_=whh_v[2])
         for g in range(4, GROUPS):
@@ -88,10 +89,11 @@ def tile_lstmlayer_kernel(tc, x, h0, c0, noise, w_ih, w_hh, b_ih, b_hh, out_h, o
 
         def grouped_for(key):
             if key not in grouped_tiles:
-                grouped_tiles[key] = work.tile([P, 4 * I], BF16, name="grouped", align_bytes=64)
+                grouped_tiles[key] = work.tile([P, 4 * I], BF16, name="grouped", bufs=4, align_bytes=64)
             return grouped_tiles[key]
 
-        whh_t = [keep.tile([P, 4, CHUNKS, P], BF16, name="whh_t%d" % j) for j in range(CHUNKS)]
+        whh_pair = [keep.tile([P, 4, CHUNKS, P], BF16, name="whh_t%d" % n) for n in range(2)]
+        whh_t = [whh_pair[j % 2] for j in range(CHUNKS)]
         base = [keep.tile([P, 4, P], F32, name="base%d" % j) for j in range(CHUNKS)]
         h0_t = keep.tile([P, CHUNKS, P], BF16, name="h0_t")
         c_last = keep.tile([P, H], F32, name="c_last")
@@ -116,7 +118,7 @@ def tile_lstmlayer_kernel(tc, x, h0, c0, noise, w_ih, w_hh, b_ih, b_hh, out_h, o
             bank = psum.tile([P, 2, CHUNKS, P], BF16, name="bank_whh", tag=tag, bufs=bufs)
             for r in range(2):
                 for kc in range(CHUNKS):
-                    nc.tensor.matmul(bank[:, r, kc, :], lhsT=whh_sb[j][:, 2 * half + r, kc * P:(kc + 1) * P], rhs=ident_b[:], start=True, stop=True)
+                    nc.tensor.matmul(bank[:, r, kc, :], lhsT=whh_sb[j][:, 2 * half + r, kc * P:(kc + 1) * P], rhs=ident_b[:], is_transpose=j >= 2, start=True, stop=True)
             return lambda engine: copy_on(engine, whh_t[j][:, 2 * half:2 * half + 2], bank[:])
 
         def base_gates(j, half, tag="prep", bufs=2):
@@ -165,9 +167,22 @@ def tile_lstmlayer_kernel(tc, x, h0, c0, noise, w_ih, w_hh, b_ih, b_hh, out_h, o
             nc.vector.tensor_tensor(out=pre[s, gate][:], in0=over_steps(base[j][:, gate, :]),
                                     in1=gate_bank[s, gate][:], op=ALU.add)
 
+        left, right = {}, {}
+
+        def factor(side, tick, slot):
+            tiles, name = (left, "left") if side == 0 else (right, "right")
+            if tick not in tiles:
+                tiles[tick] = work.tile([P, 2, STEPS, P], F32, name=name, bufs=4)
+            return tiles[tick][:, slot]
+
         def activate(s, gate):
-            act[s, gate] = work.tile([P, STEPS, P], F32, name="act", tag="act%d" % gate, bufs=5 if gate == GATE_O else 3)
-            nc.scalar.activation(out=act[s, gate][:], in_=pre[s, gate][:],
+            if gate == GATE_F:
+                act[s, gate] = work.tile([P, STEPS, P], F32, name="act_f")[:]
+            elif gate == GATE_O:
+                act[s, gate] = factor(0, s + LAG, 1)
+            else:
+                act[s, gate] = factor(0 if gate == GATE_I else 1, s + 1, 0)
+            nc.scalar.activation(out=act[s, gate], in_=pre[s, gate][:],
                                  func=ACT.Tanh if gate == GATE_G else ACT.Sigmoid)
 
         def forget(s):
@@ -176,22 +191,27 @@ def tile_lstmlayer_kernel(tc, x, h0, c0, noise, w_ih, w_hh, b_ih, b_hh, out_h, o
             nc.vector.tensor_tensor(out=prod_f[s][:], in0=act[s, GATE_F][:], in1=over_steps(consts[:, 0, j, :]), op=ALU.mult)
 
         def admit(s, engine):
-            prod_i[s] = work.tile([P, STEPS, P], F32, name="prod_i")
+            prod_i[s] = work.tile([P, STEPS, P], F32, name="prod_i", bufs=2)
             engine.tensor_tensor(out=prod_i[s][:], in0=act[s, GATE_I][:], in1=act[s, GATE_G][:], op=ALU.mult)
+
+        def products(tick):
+            both = work.tile([P, 2, STEPS, P], F32, name="both", bufs=3)
+            nc.gpsimd.tensor_tensor(out=both[:], in0=left[tick][:], in1=right[tick][:], op=ALU.mult)
+            prod_i[tick - 1] = both[:, 0]
+            h_raw[tick - LAG] = both[:, 1]
 
         def sum_cell(s, tag="cell"):
             c_bank[s] = psum.tile([P, STEPS, P], F32, name="bank_c", tag=tag, bufs=1)
             for t in range(STEPS):
-                nc.tensor.matmul(c_bank[s][:, t, :], lhsT=prod_f[s][:, t, :], rhs=ident_f[:], is_transpose=True, start=True, stop=False)
-                nc.tensor.matmul(c_bank[s][:, t, :], lhsT=prod_i[s][:, t, :], rhs=ident_f[:], is_transpose=True, start=False, stop=True)
+                nc.tensor.matmul(c_bank[s][:, t, :], lhsT=prod_f[s][:, t, :], rhs=ident_f[:], is_transpose=t > 0 or s >= UNITS - 2, start=True, stop=False)
+                nc.tensor.matmul(c_bank[s][:, t, :], lhsT=prod_i[s][:, t, :], rhs=ident_f[:], is_transpose=t < STEPS - 1 or s >= UNITS - 2, start=False, stop=True)
 
         def squash_cell(s):
             j, g = order[s]
-            tanh_c[s] = work.tile([P, STEPS, P], F32, name="tanh_c")
+            tanh_c[s] = factor(1, s + LAG, 1)
             nc.scalar.activation(out=tanh_c[s][:], in_=c_bank[s][:], func=ACT.Tanh)
             if g == GROUPS - 1:
                 nc.scalar.copy(out=c_last[:, j * P:(j + 1) * P], in_=c_bank[s][:, STEPS - 1, :])
-                nc.sync.dma_start(out=out_state[1, :, j * P:(j + 1) * P], in_=c_last[:, j * P:(j + 1) * P])
 
         def emit(s, engine):
             h_raw[s] = work.tile([P, STEPS, P], F32, name="h_raw")
@@ -209,137 +229,149 @@ def tile_lstmlayer_kernel(tc, x, h0, c0, noise, w_ih, w_hh, b_ih, b_hh, out_h, o
             if g == GROUPS - 1:
                 nc.sync.dma_start(out=out_state[0, :, cols], in_=h_out[:, STEPS - 1, :])
 
+        def turn_x(g, half, tag="prep", bufs=2):
+            return turn_words(x_sb[g], grouped_for(("x", g)), half, tag, bufs)
+
+        def turn_wih(j, half, tag="prep", bufs=2):
+            return turn_words(wih_sb[j], grouped_for(("w", j)), half, tag, bufs)
+
+        def quantize_x(g):
+            quantize(grouped_for(("x", g)), x_codes[g], x_scales[g])
+
+        def quantize_wih(j, lo=0, hi=4):
+            quantize(grouped_for(("w", j)), w_codes[j], w_scales[j], lo, hi)
+
+        def gate_step(s, gate):
+            add_base(s, gate)
+            activate(s, gate)
+
+        turn_x(0, 0)("scalar")
         bank_h0 = psum.tile([P, CHUNKS, P], BF16, name="bank_h0", tag="cell", bufs=1)
         for kc in range(CHUNKS):
             nc.tensor.matmul(bank_h0[:, kc, :], lhsT=h0_sb[:, kc * P:(kc + 1) * P], rhs=ident_b[:], start=True, stop=True)
         nc.scalar.copy(out=h0_t[:], in_=bank_h0[:])
         turn_whh(0, 0, "gate2", 1)("vector")
-        turn_words(x_sb[0], grouped_for(("x", 0)), 0)("scalar")
-        turn_words(x_sb[0], grouped_for(("x", 0)), 1)("vector")
+        turn_x(0, 1)("vector")
+        turn_wih(0, 0, "gate3", 1)("scalar")
         base_gates(0, 0, "cell", 1)("scalar")
-        turn_words(wih_sb[0], grouped_for(("w", 0)), 0, "gate3", 1)("scalar")
-        quantize(grouped_for(("x", 0)), x_codes[0], x_scales[0])
-        turn_whh(0, 1, "gate2", 1)("vector")
-        turn_words(wih_sb[0], grouped_for(("w", 0)), 1)("scalar")
-        quantize(grouped_for(("w", 0)), w_codes[0], w_scales[0], 0, 2)
-        base_gates(0, 1, "cell", 1)("scalar")
+        quantize_x(0)
+        quantize_wih(0, 0, 2)
+        turn_whh(0, 1, "gate2", 1)("scalar")
+        turn_wih(0, 1)("vector")
         project(0, (GATE_F, GATE_I))
-        quantize(grouped_for(("w", 0)), w_codes[0], w_scales[0], 2, 4)
-        turn_words(x_sb[1], grouped_for(("x", 1)), 0)("scalar")
-        project(0, (GATE_G, GATE_O))
-        copy_x = turn_words(x_sb[1], grouped_for(("x", 1)), 1)
-        add_base(0, GATE_F)
-        activate(0, GATE_F)
+        gate_step(0, GATE_F)
+        quantize_wih(0, 2, 4)
         add_base(0, GATE_I)
+        turn_x(1, 0)("vector")
+        base_gates(0, 1, "cell", 1)("scalar")
+        turn_x(1, 1)("scalar")
         activate(0, GATE_I)
-        add_base(0, GATE_G)
-        copy_x("vector")
-        activate(0, GATE_G)
+        project(0, (GATE_G, GATE_O))
+        copy_x = turn_x(2, 0)
         copy_h = turn_whh(1, 0, "cell", 1)
-        copy_w = turn_words(wih_sb[1], grouped_for(("w", 1)), 0)
+        gate_step(0, GATE_G)
+        quantize_x(1)
+        copy_x("scalar")
+        gate_step(0, GATE_O)
+        project(1, (GATE_F, GATE_I))
+        turn_x(2, 1)("scalar")
         consts = psum.tile([P, 2, CHUNKS, P], BF16, name="consts", tag="consts", bufs=1)
         for j in range(CHUNKS):
             nc.tensor.matmul(consts[:, 0, j, :], lhsT=c0_sb[:, j * P:(j + 1) * P], rhs=ident_b[:], start=True, stop=True)
         nc.tensor.matmul(consts[:, 1].rearrange("p j c -> p (j c)"), lhsT=ident_b[:], rhs=noise_sb[:], start=True, stop=True)
-        add_base(0, GATE_O)
-        quantize(grouped_for(("x", 1)), x_codes[1], x_scales[1])
-        copy_h("vector")
-        copy_w("scalar")
-        copy_w = turn_words(wih_sb[1], grouped_for(("w", 1)), 1)
-        admit(0, nc.gpsimd)
-        project(1, (GATE_F, GATE_I))
-        copy_h = turn_whh(1, 1)
         project(1, (GATE_G, GATE_O))
-        copy_w("scalar")
-        activate(0, GATE_O)
-        forget(0)
-        add_base(1, GATE_F)
-        copy_h("scalar")
-        activate(1, GATE_F)
-        quantize(grouped_for(("w", 1)), w_codes[1], w_scales[1])
-        copy_b = base_gates(1, 0)
-        sum_cell(0)
-        add_base(1, GATE_I)
-        activate(1, GATE_I)
-        copy_b("vector")
-        copy_b = base_gates(1, 1)
+        admit(0, nc.gpsimd)
+        gate_step(1, GATE_F)
+        gate_step(1, GATE_I)
+        copy_h("vector")
+        copy_h = turn_whh(1, 1, "cell", 1)
+        copy_w = turn_wih(1, 0)
+        quantize_x(2)
         project(2, (GATE_F, GATE_I))
-        add_base(1, GATE_G)
-        activate(1, GATE_G)
-        add_base(1, GATE_O)
-        copy_x = turn_words(x_sb[2], grouped_for(("x", 2)), 0)
+        copy_w2 = turn_wih(1, 1)
+        gate_step(1, GATE_G)
+        copy_h("vector")
+        forget(0)
+        copy_w("scalar")
+        copy_w2("scalar")
+        gate_step(1, GATE_O)
+        sum_cell(0)
+        copy_b = base_gates(1, 0)
         project(2, (GATE_G, GATE_O))
-        copy_b("vector")
-        activate(1, GATE_O)
         admit(1, nc.gpsimd)
+        copy_b2 = base_gates(1, 1)
+        gate_step(2, GATE_F)
         squash_cell(0)
-        emit(0, nc.gpsimd)
-        add_base(2, GATE_F)
-        copy_x("scalar")
-        copy_x = turn_words(x_sb[2], grouped_for(("x", 2)), 1)
-        activate(2, GATE_F)
-        add_base(2, GATE_I)
-        activate(2, GATE_I)
-        project(3, (GATE_F, GATE_I))
+        gate_step(2, GATE_I)
+        quantize_wih(1)
         forget(1)
+        project(3, (GATE_F, GATE_I))
+        copy_b("vector")
+        gate_step(2, GATE_G)
         sum_cell(1)
-        add_base(2, GATE_G)
-        copy_x("scalar")
-        activate(2, GATE_G)
-        add_base(2, GATE_O)
-        activate(2, GATE_O)
+        copy_b2("vector")
+        copy_x = turn_x(3, 0)
+        gate_step(2, GATE_O)
         project(3, (GATE_G, GATE_O))
-        quantize(grouped_for(("x", 2)), x_codes[2], x_scales[2])
-        copies = [turn_words(x_sb[3], grouped_for(("x", 3)), 0)]
+        copies = [(copy_x, "scalar"), (turn_x(3, 1), "scalar")]
         jobs = {s: [] for s in range(UNITS)}
         quants = {14: ("w", 2), 22: ("w", 3)}
         for g in range(3, GROUPS):
-            for half in range(1 if g == 3 else 0, 2):
-                jobs[max(2 * g - 4 + half, 3)].append(lambda g=g, half=half: turn_words(x_sb[g], grouped_for(("x", g)), half))
+            for half in range(2 if g == 3 else 0, 2):
+                jobs[2 * g - 5 + half].append(lambda g=g, half=half: (turn_x(g, half), "scalar"))
             quants[2 * g - 2] = ("x", g)
-        for j, ticks in ((2, (4, 6, 8, 10, 11, 12)), (3, (15, 16, 17, 18, 19, 20))):
+        for j, ticks in ((2, (7, 9, 13, 14, 11, 12)), (3, (15, 17, 21, 22, 19, 20))):
             for half in range(2):
-                jobs[ticks[half]].append(lambda j=j, half=half: turn_whh(j, half))
-                jobs[ticks[2 + half]].append(lambda j=j, half=half: base_gates(j, half))
-                jobs[ticks[4 + half]].append(lambda j=j, half=half: turn_words(wih_sb[j], grouped_for(("w", j)), half))
-        for s in range(3, UNITS):
+                jobs[ticks[half]].append(lambda j=j, half=half: (turn_whh(j, half), "scalar"))
+                jobs[ticks[2 + half]].append(lambda j=j, half=half: (base_gates(j, half), "vector"))
+                jobs[ticks[4 + half]].append(lambda j=j, half=half: (turn_wih(j, half), "scalar"))
+        for s in range(3, UNITS - 1):
             noise_on_vector = s % 2 == 0
-            admit(s - 1, nc.gpsimd)
-            if s >= 2:
-                squash_cell(s - 2)
-                emit(s - 2, nc.gpsimd)
-            if s >= 3 and not noise_on_vector:
-                add_noise_and_store(s - 3, False)
-            add_base(s, GATE_F)
-            activate(s, GATE_F)
-            add_base(s, GATE_I)
-            activate(s, GATE_I)
-            if s + 1 < UNITS:
-                project(s + 1, (GATE_F, GATE_I))
-            for copy in copies:
-                copy("scalar")
-            forget(s - 1)
-            sum_cell(s - 1)
-            add_base(s, GATE_G)
-            activate(s, GATE_G)
-            add_base(s, GATE_O)
-            activate(s, GATE_O)
-            if s + 1 < UNITS:
-                project(s + 1, (GATE_G, GATE_O))
-            if s >= 3 and noise_on_vector:
-                add_noise_and_store(s - 3, True)
+            if s >= 4 and not noise_on_vector:
+                add_noise_and_store(s - 4, False)
+            products(s)
+            gate_step(s, GATE_F)
             if s in quants:
                 kind, n = quants[s]
                 quantize(grouped_for(quants[s]), (x_codes if kind == "x" else w_codes)[n], (x_scales if kind == "x" else w_scales)[n])
+            gate_step(s, GATE_I)
+            squash_cell(s - 2)
+            project(s + 1, (GATE_F, GATE_I))
+            for copy, engine in copies:
+                if engine == "scalar":
+                    copy(engine)
+            forget(s - 1)
+            gate_step(s, GATE_G)
+            gate_step(s, GATE_O)
+            for copy, engine in copies:
+                if engine == "vector":
+                    copy(engine)
+            project(s + 1, (GATE_G, GATE_O))
+            if s >= 4 and noise_on_vector:
+                add_noise_and_store(s - 4, True)
+            sum_cell(s - 1)
             copies = [job() for job in jobs[s]]
         last = UNITS - 1
+        emit(last - 3, nc.gpsimd)
+        admit(last - 1, nc.gpsimd)
+        for gate in (GATE_F, GATE_I, GATE_G):
+            gate_step(last, gate)
+        squash_cell(last - 2)
+        forget(last - 1)
+        sum_cell(last - 1, "gate0")
         forget(last)
         admit(last, nc.vector)
-        squash_cell(last - 1)
         sum_cell(last, "gate1")
+        emit(last - 2, nc.gpsimd)
+        add_base(last, GATE_O)
+        add_noise_and_store(last - 4, True)
+        add_noise_and_store(last - 3, True)
+        squash_cell(last - 1)
+        activate(last, GATE_O)
         emit(last - 1, nc.gpsimd)
         add_noise_and_store(last - 2, True)
         squash_cell(last)
-        add_noise_and_store(last - 1, True)
+        nc.sync.dma_start(out=out_state[1], in_=c_last[:])
         emit(last, nc.vector)
+        add_noise_and_store(last - 1, True)
         add_noise_and_store(last, True)

@@ -15,19 +15,26 @@ ACT = mybir.ActivationFunctionType
 ALU = mybir.AluOpType
 
 P = 128
+GATES = 4
+GATE_I, GATE_F, GATE_G, GATE_O = 0, 1, 2, 3
 STEPS = 4
 GROUPS = T // STEPS
 CHUNKS = H // P
 UNITS = GROUPS * CHUNKS
-GATE_I, GATE_F, GATE_G, GATE_O = 0, 1, 2, 3
-LAG = 3
-GATE_ORDER = (GATE_F, GATE_I, GATE_G, GATE_O)
+HEAD_TICKS = 3
+EMIT_LAG = 3
+NOISE_LAG = EMIT_LAG + 1
+QUANTIZE_LEAD = 2
+INPUT_LEADS = (5, 4)
+WIH_LEADS, WHH_LEADS, BASE_LEADS = (9, 7), (5, 4), (3, 2)
 
 
 def tile_lstmlayer_kernel(tc, x, h0, c0, noise, w_ih, w_hh, b_ih, b_hh, out_h, out_state):
     nc = tc.nc
-    order = [(j, g) for j in (0, 1) for g in range(3)] + [(j, g) for g in range(3, GROUPS) for j in (0, 1)]
+    order = [(j, g) for j in (0, 1) for g in range(HEAD_TICKS)]
+    order += [(j, g) for g in range(HEAD_TICKS, GROUPS) for j in (0, 1)]
     order += [(j, g) for j in (2, 3) for g in range(GROUPS)]
+    last = UNITS - 1
     with ExitStack() as ctx:
         keep = ctx.enter_context(tc.tile_pool(name="keep", bufs=1))
         work = ctx.enter_context(tc.tile_pool(name="work", bufs=3))
@@ -37,54 +44,59 @@ def tile_lstmlayer_kernel(tc, x, h0, c0, noise, w_ih, w_hh, b_ih, b_hh, out_h, o
         ident_f = keep.tile([P, P], F32, name="ident_f")
         ident_b = keep.tile([P, P], BF16, name="ident_b")
         ones_b = keep.tile([P, P], BF16, name="ones_b")
-        bias_rows = keep.tile([P, 4 * H], BF16, name="bias_rows")
+        bias_rows = keep.tile([P, GATES * H], BF16, name="bias_rows")
         nc.vector.memset(bias_rows[:], 0.0)
         make_identity(nc, ident_b[:])
         make_identity(nc, ident_f[:])
         nc.vector.memset(ones_b[:], 1.0)
 
         x_sb = [keep.tile([P, STEPS, I], BF16, name="x_sb%d" % g) for g in range(GROUPS)]
-        wih_sb = [keep.tile([P, 4, I], BF16, name="wih_sb%d" % j) for j in range(CHUNKS)]
-        whh_sb = [keep.tile([P, 4, H], BF16, name="whh_sb%d" % j) for j in range(CHUNKS)]
+        wih_sb = [keep.tile([P, GATES, I], BF16, name="wih_sb%d" % j) for j in range(CHUNKS)]
+        whh_sb = [keep.tile([P, GATES, H], BF16, name="whh_sb%d" % j) for j in range(CHUNKS)]
         h0_sb = keep.tile([P, H], BF16, name="h0_sb")
         c0_sb = keep.tile([P, H], BF16, name="c0_sb")
         noise_sb = keep.tile([P, H], BF16, name="noise_sb")
-        wih_v = w_ih.rearrange("(g j p) k -> j p g k", g=4, j=CHUNKS)
-        whh_v = w_hh.rearrange("(g j p) k -> j p g k", g=4, j=CHUNKS)
+        x_v = x.rearrange("(g t) b k -> g b t k", t=STEPS)
+        wih_v = w_ih.rearrange("(q j p) k -> j p q k", q=GATES, j=CHUNKS)
+        whh_v = w_hh.rearrange("(q j p) k -> j p q k", q=GATES, j=CHUNKS)
 
-        def load_x(g):
-            nc.sync.dma_start(out=x_sb[g][:], in_=x[g * STEPS:(g + 1) * STEPS].rearrange("t b k -> b t k"))
+        def load(dst, src):
+            nc.sync.dma_start(out=dst, in_=src)
 
-        x0_v = x[0:STEPS].rearrange("t b k -> b t k")
-        x1_v = x[STEPS:2 * STEPS].rearrange("t b k -> b t k")
-        nc.sync.dma_start(out=x_sb[0][:, 0:2], in_=x0_v[:, 0:2])
-        nc.sync.dma_start(out=h0_sb[:], in_=h0)
-        nc.sync.dma_start(out=whh_sb[0][:, 0:2], in_=whh_v[0][:, 0:2])
+        def load_half(tiles, view, n, half):
+            load(tiles[n][:, 2 * half:2 * half + 2], view[n][:, 2 * half:2 * half + 2])
+
+        load_half(x_sb, x_v, 0, 0)
+        load(h0_sb[:], h0)
+        load_half(whh_sb, whh_v, 0, 0)
         nc.scalar.dma_start(out=bias_rows[0:1, :], in_=b_ih.rearrange("(o n) -> o n", o=1))
         nc.scalar.dma_start(out=bias_rows[1:2, :], in_=b_hh.rearrange("(o n) -> o n", o=1))
-        nc.sync.dma_start(out=x_sb[0][:, 2:4], in_=x0_v[:, 2:4])
-        nc.sync.dma_start(out=wih_sb[0][:, 0:2], in_=wih_v[0][:, 0:2])
-        nc.sync.dma_start(out=whh_sb[0][:, 2:4], in_=whh_v[0][:, 2:4])
-        nc.sync.dma_start(out=wih_sb[0][:, 2:4], in_=wih_v[0][:, 2:4])
-        nc.sync.dma_start(out=c0_sb[:], in_=c0)
-        nc.sync.dma_start(out=noise_sb[:], in_=noise)
-        nc.sync.dma_start(out=x_sb[1][:, 0:2], in_=x1_v[:, 0:2])
-        nc.sync.dma_start(out=x_sb[1][:, 2:4], in_=x1_v[:, 2:4])
-        load_x(2)
-        nc.sync.dma_start(out=whh_sb[1][:], in_=whh_v[1])
-        nc.sync.dma_start(out=wih_sb[1][:], in_=wih_v[1])
-        load_x(3)
-        nc.sync.dma_start(out=whh_sb[2][:], in_=whh_v[2])
+        load_half(x_sb, x_v, 0, 1)
+        load_half(wih_sb, wih_v, 0, 0)
+        load_half(whh_sb, whh_v, 0, 1)
+        load_half(wih_sb, wih_v, 0, 1)
+        load_half(x_sb, x_v, 1, 0)
+        load_half(x_sb, x_v, 1, 1)
+        load(c0_sb[:], c0)
+        load_half(x_sb, x_v, 2, 0)
+        load_half(x_sb, x_v, 2, 1)
+        load_half(whh_sb, whh_v, 1, 0)
+        load(noise_sb[:], noise)
+        load_half(whh_sb, whh_v, 1, 1)
+        load_half(wih_sb, wih_v, 1, 0)
+        load_half(wih_sb, wih_v, 1, 1)
+        load(x_sb[3][:], x_v[3])
+        load(whh_sb[2][:], whh_v[2])
         for g in range(4, GROUPS):
-            load_x(g)
-        nc.sync.dma_start(out=wih_sb[2][:], in_=wih_v[2])
-        nc.sync.dma_start(out=whh_sb[3][:], in_=whh_v[3])
-        nc.sync.dma_start(out=wih_sb[3][:], in_=wih_v[3])
+            load(x_sb[g][:], x_v[g])
+        load(wih_sb[2][:], wih_v[2])
+        load(whh_sb[3][:], whh_v[3])
+        load(wih_sb[3][:], wih_v[3])
 
         x_codes = [keep.tile([P, STEPS * P], U32, name="x_codes%d" % g, align_bytes=64) for g in range(GROUPS)]
         x_scales = [keep.tile([P, STEPS * P], U8, name="x_scales%d" % g, align_bytes=64) for g in range(GROUPS)]
-        w_codes = [keep.tile([P, 4 * P], U32, name="w_codes%d" % j, align_bytes=64) for j in range(CHUNKS)]
-        w_scales = [keep.tile([P, 4 * P], U8, name="w_scales%d" % j, align_bytes=64) for j in range(CHUNKS)]
+        w_codes = [keep.tile([P, GATES * P], U32, name="w_codes%d" % j, align_bytes=64) for j in range(CHUNKS)]
+        w_scales = [keep.tile([P, GATES * P], U8, name="w_scales%d" % j, align_bytes=64) for j in range(CHUNKS)]
         grouped_tiles = {}
 
         def grouped_for(key):
@@ -92,9 +104,9 @@ def tile_lstmlayer_kernel(tc, x, h0, c0, noise, w_ih, w_hh, b_ih, b_hh, out_h, o
                 grouped_tiles[key] = work.tile([P, 4 * I], BF16, name="grouped", bufs=4, align_bytes=64)
             return grouped_tiles[key]
 
-        whh_pair = [keep.tile([P, 4, CHUNKS, P], BF16, name="whh_t%d" % n) for n in range(2)]
+        whh_pair = [keep.tile([P, GATES, CHUNKS, P], BF16, name="whh_t%d" % n) for n in range(2)]
         whh_t = [whh_pair[j % 2] for j in range(CHUNKS)]
-        base = [keep.tile([P, 4, P], F32, name="base%d" % j) for j in range(CHUNKS)]
+        base = [keep.tile([P, GATES, P], F32, name="base%d" % j) for j in range(CHUNKS)]
         h0_t = keep.tile([P, CHUNKS, P], BF16, name="h0_t")
         c_last = keep.tile([P, H], F32, name="c_last")
 
@@ -104,9 +116,12 @@ def tile_lstmlayer_kernel(tc, x, h0, c0, noise, w_ih, w_hh, b_ih, b_hh, out_h, o
             else:
                 nc.scalar.copy(out=out, in_=in_)
 
-        def turn_words(src, grouped, half, tag="prep", bufs=2):
+        def bank_for(shape, dtype, name, tag):
+            return psum.tile(shape, dtype, name=name, tag=tag, bufs=2 if tag == "prep" else 1)
+
+        def turn_words(src, grouped, half, tag):
             words = src[:].rearrange("p q k -> p (q k)").bitcast(F32)
-            bank = psum.tile([P, 2, 2, P], F32, name="bank_words", tag=tag, bufs=bufs)
+            bank = bank_for([P, 2, 2, P], F32, "bank_words", tag)
             for r in range(2):
                 w0 = (2 * half + r) * (I // 2)
                 for u in range(2):
@@ -114,15 +129,22 @@ def tile_lstmlayer_kernel(tc, x, h0, c0, noise, w_ih, w_hh, b_ih, b_hh, out_h, o
             dst = grouped[:].bitcast(F32).rearrange("p (q c u) -> p q c u", q=4, u=2)[:, 2 * half:2 * half + 2]
             return lambda engine: copy_on(engine, dst, bank[:].rearrange("p r u c -> p r c u"))
 
-        def turn_whh(j, half, tag="prep", bufs=2):
-            bank = psum.tile([P, 2, CHUNKS, P], BF16, name="bank_whh", tag=tag, bufs=bufs)
+        def turn_x(g, half):
+            return turn_words(x_sb[g], grouped_for(("x", g)), half, "prep")
+
+        def turn_wih(j, half, tag="prep"):
+            return turn_words(wih_sb[j], grouped_for(("w", j)), half, tag)
+
+        def turn_whh(j, half, tag="prep"):
+            bank = bank_for([P, 2, CHUNKS, P], BF16, "bank_whh", tag)
             for r in range(2):
                 for kc in range(CHUNKS):
-                    nc.tensor.matmul(bank[:, r, kc, :], lhsT=whh_sb[j][:, 2 * half + r, kc * P:(kc + 1) * P], rhs=ident_b[:], is_transpose=j >= 2, start=True, stop=True)
+                    nc.tensor.matmul(bank[:, r, kc, :], lhsT=whh_sb[j][:, 2 * half + r, kc * P:(kc + 1) * P], rhs=ident_b[:],
+                                     is_transpose=j >= 2, start=True, stop=True)
             return lambda engine: copy_on(engine, whh_t[j][:, 2 * half:2 * half + 2], bank[:])
 
-        def base_gates(j, half, tag="prep", bufs=2):
-            bank = psum.tile([P, 2, P], F32, name="bank_base", tag=tag, bufs=bufs)
+        def base_gates(j, half, tag="prep"):
+            bank = bank_for([P, 2, P], F32, "bank_base", tag)
             for r in range(2):
                 gate = 2 * half + r
                 bias = bias_rows[:, gate * H + j * P:gate * H + (j + 1) * P]
@@ -132,15 +154,22 @@ def tile_lstmlayer_kernel(tc, x, h0, c0, noise, w_ih, w_hh, b_ih, b_hh, out_h, o
                     nc.tensor.matmul(bank[:, r, :], lhsT=lhsT, rhs=rhs, start=(n == 0), stop=(n == len(pairs) - 1))
             return lambda engine: copy_on(engine, base[j][:, 2 * half:2 * half + 2], bank[:])
 
-        def quantize(grouped, codes, scales, lo=0, hi=4):
-            nc.vector.quantize_mx(out=codes[:, lo * P:hi * P].bitcast(E5M2X4), scales=scales[:, lo * P:hi * P], in_=grouped[:, lo * I:hi * I])
+        def quantize(grouped, codes, scales, lo, hi):
+            nc.vector.quantize_mx(out=codes[:, lo * P:hi * P].bitcast(E5M2X4), scales=scales[:, lo * P:hi * P],
+                                  in_=grouped[:, lo * I:hi * I])
+
+        def quantize_x(g):
+            quantize(grouped_for(("x", g)), x_codes[g], x_scales[g], 0, STEPS)
+
+        def quantize_wih(j, lo=0, hi=GATES):
+            quantize(grouped_for(("w", j)), w_codes[j], w_scales[j], lo, hi)
 
         gate_bank, pre, act, prod_f, prod_i, c_bank, tanh_c, h_raw = {}, {}, {}, {}, {}, {}, {}, {}
 
-        def project(s, gates=GATE_ORDER):
+        def project(s, gates):
             j, g = order[s]
             for gate in gates:
-                bank = psum.tile([P, STEPS, P], F32, name="bank_gate", tag="gate%d" % gate, bufs=1)
+                bank = bank_for([P, STEPS, P], F32, "bank_gate", "gate%d" % gate)
                 cols = slice(gate * P, (gate + 1) * P)
                 if gate == GATE_O:
                     for t in range(STEPS):
@@ -169,189 +198,188 @@ def tile_lstmlayer_kernel(tc, x, h0, c0, noise, w_ih, w_hh, b_ih, b_hh, out_h, o
 
         left, right = {}, {}
 
-        def factor(side, tick, slot):
-            tiles, name = (left, "left") if side == 0 else (right, "right")
+        def factor(tiles, name, tick, part):
             if tick not in tiles:
-                tiles[tick] = work.tile([P, 2, STEPS, P], F32, name=name, bufs=4)
-            return tiles[tick][:, slot]
+                tiles[tick] = work.tile([P, 2, STEPS, P], F32, name=name, bufs=EMIT_LAG + 1)
+            return tiles[tick][:, part]
 
         def activate(s, gate):
             if gate == GATE_F:
                 act[s, gate] = work.tile([P, STEPS, P], F32, name="act_f")[:]
-            elif gate == GATE_O:
-                act[s, gate] = factor(0, s + LAG, 1)
+            elif gate == GATE_I:
+                act[s, gate] = factor(left, "left", s + 1, 0)
+            elif gate == GATE_G:
+                act[s, gate] = factor(right, "right", s + 1, 0)
             else:
-                act[s, gate] = factor(0 if gate == GATE_I else 1, s + 1, 0)
+                act[s, gate] = factor(left, "left", s + EMIT_LAG, 1)
             nc.scalar.activation(out=act[s, gate], in_=pre[s, gate][:],
                                  func=ACT.Tanh if gate == GATE_G else ACT.Sigmoid)
 
+        def gate_step(s, gate):
+            add_base(s, gate)
+            activate(s, gate)
+
         def forget(s):
             j = order[s][0]
-            prod_f[s] = work.tile([P, STEPS, P], F32, name="prod_f")
-            nc.vector.tensor_tensor(out=prod_f[s][:], in0=act[s, GATE_F][:], in1=over_steps(consts[:, 0, j, :]), op=ALU.mult)
+            prod_f[s] = work.tile([P, STEPS, P], F32, name="prod_f")[:]
+            nc.vector.tensor_tensor(out=prod_f[s], in0=act[s, GATE_F], in1=over_steps(consts[:, 0, j, :]), op=ALU.mult)
 
         def admit(s, engine):
-            prod_i[s] = work.tile([P, STEPS, P], F32, name="prod_i", bufs=2)
-            engine.tensor_tensor(out=prod_i[s][:], in0=act[s, GATE_I][:], in1=act[s, GATE_G][:], op=ALU.mult)
+            prod_i[s] = work.tile([P, STEPS, P], F32, name="prod_i", bufs=2)[:]
+            engine.tensor_tensor(out=prod_i[s], in0=act[s, GATE_I], in1=act[s, GATE_G], op=ALU.mult)
+
+        def emit(s, engine):
+            h_raw[s] = work.tile([P, STEPS, P], F32, name="h_raw")[:]
+            engine.tensor_tensor(out=h_raw[s], in0=act[s, GATE_O], in1=tanh_c[s], op=ALU.mult)
 
         def products(tick):
-            both = work.tile([P, 2, STEPS, P], F32, name="both", bufs=3)
+            both = work.tile([P, 2, STEPS, P], F32, name="both")
             nc.gpsimd.tensor_tensor(out=both[:], in0=left[tick][:], in1=right[tick][:], op=ALU.mult)
             prod_i[tick - 1] = both[:, 0]
-            h_raw[tick - LAG] = both[:, 1]
+            h_raw[tick - EMIT_LAG] = both[:, 1]
 
         def sum_cell(s, tag="cell"):
-            c_bank[s] = psum.tile([P, STEPS, P], F32, name="bank_c", tag=tag, bufs=1)
+            mx_follows = s < last - 1
+            c_bank[s] = bank_for([P, STEPS, P], F32, "bank_c", tag)
             for t in range(STEPS):
-                nc.tensor.matmul(c_bank[s][:, t, :], lhsT=prod_f[s][:, t, :], rhs=ident_f[:], is_transpose=t > 0 or s >= UNITS - 2, start=True, stop=False)
-                nc.tensor.matmul(c_bank[s][:, t, :], lhsT=prod_i[s][:, t, :], rhs=ident_f[:], is_transpose=t < STEPS - 1 or s >= UNITS - 2, start=False, stop=True)
+                nc.tensor.matmul(c_bank[s][:, t, :], lhsT=prod_f[s][:, t, :], rhs=ident_f[:],
+                                 is_transpose=not (mx_follows and t == 0), start=True, stop=False)
+                nc.tensor.matmul(c_bank[s][:, t, :], lhsT=prod_i[s][:, t, :], rhs=ident_f[:],
+                                 is_transpose=not (mx_follows and t == STEPS - 1), start=False, stop=True)
 
         def squash_cell(s):
             j, g = order[s]
-            tanh_c[s] = factor(1, s + LAG, 1)
-            nc.scalar.activation(out=tanh_c[s][:], in_=c_bank[s][:], func=ACT.Tanh)
+            tanh_c[s] = factor(right, "right", s + EMIT_LAG, 1)
+            nc.scalar.activation(out=tanh_c[s], in_=c_bank[s][:], func=ACT.Tanh)
             if g == GROUPS - 1:
                 nc.scalar.copy(out=c_last[:, j * P:(j + 1) * P], in_=c_bank[s][:, STEPS - 1, :])
-
-        def emit(s, engine):
-            h_raw[s] = work.tile([P, STEPS, P], F32, name="h_raw")
-            engine.tensor_tensor(out=h_raw[s][:], in0=act[s, GATE_O][:], in1=tanh_c[s][:], op=ALU.mult)
 
         def add_noise_and_store(s, on_vector):
             j, g = order[s]
             cols = slice(j * P, (j + 1) * P)
             h_out = work.tile([P, STEPS, P], F32, name="h_out", bufs=6)
             if on_vector:
-                nc.vector.tensor_tensor(out=h_out[:], in0=h_raw[s][:], in1=over_steps(consts[:, 1, j, :]), op=ALU.add)
+                nc.vector.tensor_tensor(out=h_out[:], in0=h_raw[s], in1=over_steps(consts[:, 1, j, :]), op=ALU.add)
             else:
-                nc.gpsimd.tensor_tensor(out=h_out[:], in0=h_raw[s][:], in1=over_steps(noise_sb[:, cols]), op=ALU.add)
+                nc.gpsimd.tensor_tensor(out=h_out[:], in0=h_raw[s], in1=over_steps(noise_sb[:, cols]), op=ALU.add)
+            if g == GROUPS - 1:
+                nc.sync.dma_start(out=out_state[1, :, cols], in_=c_last[:, cols])
             nc.sync.dma_start(out=out_h[g * STEPS:(g + 1) * STEPS, :, cols].rearrange("t b c -> b t c"), in_=h_out[:])
             if g == GROUPS - 1:
                 nc.sync.dma_start(out=out_state[0, :, cols], in_=h_out[:, STEPS - 1, :])
 
-        def turn_x(g, half, tag="prep", bufs=2):
-            return turn_words(x_sb[g], grouped_for(("x", g)), half, tag, bufs)
-
-        def turn_wih(j, half, tag="prep", bufs=2):
-            return turn_words(wih_sb[j], grouped_for(("w", j)), half, tag, bufs)
-
-        def quantize_x(g):
-            quantize(grouped_for(("x", g)), x_codes[g], x_scales[g])
-
-        def quantize_wih(j, lo=0, hi=4):
-            quantize(grouped_for(("w", j)), w_codes[j], w_scales[j], lo, hi)
-
-        def gate_step(s, gate):
-            add_base(s, gate)
-            activate(s, gate)
-
         turn_x(0, 0)("scalar")
-        bank_h0 = psum.tile([P, CHUNKS, P], BF16, name="bank_h0", tag="cell", bufs=1)
+        bank_h0 = bank_for([P, CHUNKS, P], BF16, "bank_h0", "cell")
         for kc in range(CHUNKS):
             nc.tensor.matmul(bank_h0[:, kc, :], lhsT=h0_sb[:, kc * P:(kc + 1) * P], rhs=ident_b[:], start=True, stop=True)
         nc.scalar.copy(out=h0_t[:], in_=bank_h0[:])
-        turn_whh(0, 0, "gate2", 1)("vector")
+        turn_whh(0, 0, "gate2")("vector")
         turn_x(0, 1)("vector")
-        turn_wih(0, 0, "gate3", 1)("scalar")
-        base_gates(0, 0, "cell", 1)("scalar")
+        turn_wih(0, 0, "gate3")("scalar")
+        base_gates(0, 0, "cell")("scalar")
         quantize_x(0)
         quantize_wih(0, 0, 2)
-        turn_whh(0, 1, "gate2", 1)("scalar")
-        turn_wih(0, 1)("vector")
+        turn_whh(0, 1, "gate2")("scalar")
+        turn_wih(0, 1)("scalar")
         project(0, (GATE_F, GATE_I))
+
         gate_step(0, GATE_F)
-        quantize_wih(0, 2, 4)
+        quantize_wih(0, 2, GATES)
         add_base(0, GATE_I)
         turn_x(1, 0)("vector")
-        base_gates(0, 1, "cell", 1)("scalar")
-        turn_x(1, 1)("scalar")
+        base_gates(0, 1, "cell")("vector")
+        turn_x(1, 1)("vector")
         activate(0, GATE_I)
         project(0, (GATE_G, GATE_O))
         copy_x = turn_x(2, 0)
-        copy_h = turn_whh(1, 0, "cell", 1)
+        copy_whh = turn_whh(1, 0, "cell")
         gate_step(0, GATE_G)
         quantize_x(1)
         copy_x("scalar")
         gate_step(0, GATE_O)
         project(1, (GATE_F, GATE_I))
         turn_x(2, 1)("scalar")
-        consts = psum.tile([P, 2, CHUNKS, P], BF16, name="consts", tag="consts", bufs=1)
+        consts = bank_for([P, 2, CHUNKS, P], BF16, "consts", "consts")
         for j in range(CHUNKS):
             nc.tensor.matmul(consts[:, 0, j, :], lhsT=c0_sb[:, j * P:(j + 1) * P], rhs=ident_b[:], start=True, stop=True)
         nc.tensor.matmul(consts[:, 1].rearrange("p j c -> p (j c)"), lhsT=ident_b[:], rhs=noise_sb[:], start=True, stop=True)
         project(1, (GATE_G, GATE_O))
         admit(0, nc.gpsimd)
+
         gate_step(1, GATE_F)
         gate_step(1, GATE_I)
-        copy_h("vector")
-        copy_h = turn_whh(1, 1, "cell", 1)
-        copy_w = turn_wih(1, 0)
+        copy_whh("vector")
+        copy_whh = turn_whh(1, 1, "cell")
+        copy_wih_if = turn_wih(1, 0)
         quantize_x(2)
         project(2, (GATE_F, GATE_I))
-        copy_w2 = turn_wih(1, 1)
+        copy_wih_go = turn_wih(1, 1)
         gate_step(1, GATE_G)
-        copy_h("vector")
+        copy_whh("vector")
         forget(0)
-        copy_w("scalar")
-        copy_w2("scalar")
+        copy_wih_if("scalar")
+        copy_wih_go("scalar")
         gate_step(1, GATE_O)
         sum_cell(0)
-        copy_b = base_gates(1, 0)
+        copy_base_if = base_gates(1, 0)
         project(2, (GATE_G, GATE_O))
         admit(1, nc.gpsimd)
-        copy_b2 = base_gates(1, 1)
+
+        copy_base_go = base_gates(1, 1)
         gate_step(2, GATE_F)
         squash_cell(0)
         gate_step(2, GATE_I)
         quantize_wih(1)
         forget(1)
         project(3, (GATE_F, GATE_I))
-        copy_b("vector")
+        copy_base_if("scalar")
         gate_step(2, GATE_G)
         sum_cell(1)
-        copy_b2("vector")
+        copy_base_go("scalar")
         copy_x = turn_x(3, 0)
         gate_step(2, GATE_O)
         project(3, (GATE_G, GATE_O))
-        copies = [(copy_x, "scalar"), (turn_x(3, 1), "scalar")]
+        copies = [copy_x, turn_x(3, 1)]
+
         jobs = {s: [] for s in range(UNITS)}
-        quants = {14: ("w", 2), 22: ("w", 3)}
-        for g in range(3, GROUPS):
-            for half in range(2 if g == 3 else 0, 2):
-                jobs[2 * g - 5 + half].append(lambda g=g, half=half: (turn_x(g, half), "scalar"))
-            quants[2 * g - 2] = ("x", g)
-        for j, ticks in ((2, (7, 9, 13, 14, 11, 12)), (3, (15, 17, 21, 22, 19, 20))):
+        quantize_at = {}
+        for g in range(HEAD_TICKS, GROUPS):
+            first = order.index((0, g))
+            quantize_at[first - QUANTIZE_LEAD] = (quantize_x, g)
+            if g > HEAD_TICKS:
+                for half in range(2):
+                    jobs[first - INPUT_LEADS[half]].append((turn_x, g, half))
+        for j in (2, 3):
+            first = order.index((j, 0))
+            quantize_at[first - QUANTIZE_LEAD] = (quantize_wih, j)
             for half in range(2):
-                jobs[ticks[half]].append(lambda j=j, half=half: (turn_whh(j, half), "scalar"))
-                jobs[ticks[2 + half]].append(lambda j=j, half=half: (base_gates(j, half), "vector"))
-                jobs[ticks[4 + half]].append(lambda j=j, half=half: (turn_wih(j, half), "scalar"))
-        for s in range(3, UNITS - 1):
+                jobs[first - WHH_LEADS[half]].append((turn_whh, j, half))
+                jobs[first - BASE_LEADS[half]].append((base_gates, j, half))
+                jobs[first - WIH_LEADS[half]].append((turn_wih, j, half))
+
+        for s in range(HEAD_TICKS, last):
             noise_on_vector = s % 2 == 0
-            if s >= 4 and not noise_on_vector:
-                add_noise_and_store(s - 4, False)
+            if s >= NOISE_LAG and not noise_on_vector:
+                add_noise_and_store(s - NOISE_LAG, False)
             products(s)
             gate_step(s, GATE_F)
-            if s in quants:
-                kind, n = quants[s]
-                quantize(grouped_for(quants[s]), (x_codes if kind == "x" else w_codes)[n], (x_scales if kind == "x" else w_scales)[n])
+            if s in quantize_at:
+                quantize_operand, n = quantize_at[s]
+                quantize_operand(n)
             gate_step(s, GATE_I)
             squash_cell(s - 2)
             project(s + 1, (GATE_F, GATE_I))
-            for copy, engine in copies:
-                if engine == "scalar":
-                    copy(engine)
+            for copy in copies:
+                copy("scalar")
             forget(s - 1)
             gate_step(s, GATE_G)
             gate_step(s, GATE_O)
-            for copy, engine in copies:
-                if engine == "vector":
-                    copy(engine)
             project(s + 1, (GATE_G, GATE_O))
-            if s >= 4 and noise_on_vector:
-                add_noise_and_store(s - 4, True)
+            if s >= NOISE_LAG and noise_on_vector:
+                add_noise_and_store(s - NOISE_LAG, True)
             sum_cell(s - 1)
-            copies = [job() for job in jobs[s]]
-        last = UNITS - 1
+            copies = [job(n, half) for job, n, half in jobs[s]]
+
         emit(last - 3, nc.gpsimd)
         admit(last - 1, nc.gpsimd)
         for gate in (GATE_F, GATE_I, GATE_G):
@@ -371,7 +399,6 @@ def tile_lstmlayer_kernel(tc, x, h0, c0, noise, w_ih, w_hh, b_ih, b_hh, out_h, o
         emit(last - 1, nc.gpsimd)
         add_noise_and_store(last - 2, True)
         squash_cell(last)
-        nc.sync.dma_start(out=out_state[1], in_=c_last[:])
         emit(last, nc.vector)
         add_noise_and_store(last - 1, True)
         add_noise_and_store(last, True)

from contextlib import ExitStack

import concourse.mybir as mybir
from concourse.masks import make_identity

T, B, I, H = 32, 128, 512, 512
FLOPS = 2 * T * B * I * 4 * H + 2 * B * H * 4 * H

F32 = mybir.dt.float32
BF16 = mybir.dt.bfloat16
U32 = mybir.dt.uint32
U8 = mybir.dt.uint8
E5M2X4 = mybir.dt.float8_e5m2_x4
ACT = mybir.ActivationFunctionType
ALU = mybir.AluOpType

P = 128
GATES = 4
GATE_I, GATE_F, GATE_G, GATE_O = 0, 1, 2, 3
STEPS = 4
GROUPS = T // STEPS
CHUNKS = H // P
UNITS = GROUPS * CHUNKS
HEAD_TICKS = 3
EMIT_LAG = 3
NOISE_LAG = EMIT_LAG + 1
QUANTIZE_LEAD = 2
INPUT_LEADS = (5, 4)
WIH_LEADS, WHH_LEADS, BASE_LEADS = (9, 7), (5, 4), (3, 2)


def tile_lstmlayer_kernel(tc, x, h0, c0, noise, w_ih, w_hh, b_ih, b_hh, out_h, out_state):
    nc = tc.nc
    order = [(j, g) for j in (0, 1) for g in range(HEAD_TICKS)]
    order += [(j, g) for g in range(HEAD_TICKS, GROUPS) for j in (0, 1)]
    order += [(j, g) for j in (2, 3) for g in range(GROUPS)]
    last = UNITS - 1
    with ExitStack() as ctx:
        keep = ctx.enter_context(tc.tile_pool(name="keep", bufs=1))
        work = ctx.enter_context(tc.tile_pool(name="work", bufs=3))
        psum = ctx.enter_context(tc.psum_pool(name="psum", bufs=1))
        ctx.enter_context(tc.manual_schedule())

        ident_f = keep.tile([P, P], F32, name="ident_f")
        ident_b = keep.tile([P, P], BF16, name="ident_b")
        ones_b = keep.tile([P, P], BF16, name="ones_b")
        bias_rows = keep.tile([P, GATES * H], BF16, name="bias_rows")
        nc.vector.memset(bias_rows[:], 0.0)
        make_identity(nc, ident_b[:])
        make_identity(nc, ident_f[:])
        nc.vector.memset(ones_b[:], 1.0)

        x_sb = [keep.tile([P, STEPS, I], BF16, name="x_sb%d" % g) for g in range(GROUPS)]
        wih_sb = [keep.tile([P, GATES, I], BF16, name="wih_sb%d" % j) for j in range(CHUNKS)]
        whh_sb = [keep.tile([P, GATES, H], BF16, name="whh_sb%d" % j) for j in range(CHUNKS)]
        h0_sb = keep.tile([P, H], BF16, name="h0_sb")
        c0_sb = keep.tile([P, H], BF16, name="c0_sb")
        noise_sb = keep.tile([P, H], BF16, name="noise_sb")
        x_v = x.rearrange("(g t) b k -> g b t k", t=STEPS)
        wih_v = w_ih.rearrange("(q j p) k -> j p q k", q=GATES, j=CHUNKS)
        whh_v = w_hh.rearrange("(q j p) k -> j p q k", q=GATES, j=CHUNKS)

        def load(dst, src):
            nc.sync.dma_start(out=dst, in_=src)

        def load_half(tiles, view, n, half):
            load(tiles[n][:, 2 * half:2 * half + 2], view[n][:, 2 * half:2 * half + 2])

        load_half(x_sb, x_v, 0, 0)
        load(h0_sb[:], h0)
        load_half(whh_sb, whh_v, 0, 0)
        nc.scalar.dma_start(out=bias_rows[0:1, :], in_=b_ih.rearrange("(o n) -> o n", o=1))
        nc.scalar.dma_start(out=bias_rows[1:2, :], in_=b_hh.rearrange("(o n) -> o n", o=1))
        load_half(x_sb, x_v, 0, 1)
        load_half(wih_sb, wih_v, 0, 0)
        load_half(whh_sb, whh_v, 0, 1)
        load_half(wih_sb, wih_v, 0, 1)
        load_half(x_sb, x_v, 1, 0)
        load_half(x_sb, x_v, 1, 1)
        load(c0_sb[:], c0)
        load_half(x_sb, x_v, 2, 0)
        load_half(x_sb, x_v, 2, 1)
        load_half(whh_sb, whh_v, 1, 0)
        load(noise_sb[:], noise)
        load_half(whh_sb, whh_v, 1, 1)
        load_half(wih_sb, wih_v, 1, 0)
        load_half(wih_sb, wih_v, 1, 1)
        load(x_sb[3][:], x_v[3])
        load(whh_sb[2][:], whh_v[2])
        for g in range(4, GROUPS):
            load(x_sb[g][:], x_v[g])
        load(wih_sb[2][:], wih_v[2])
        load(whh_sb[3][:], whh_v[3])
        load(wih_sb[3][:], wih_v[3])

        x_codes = [keep.tile([P, STEPS * P], U32, name="x_codes%d" % g, align_bytes=64) for g in range(GROUPS)]
        x_scales = [keep.tile([P, STEPS * P], U8, name="x_scales%d" % g, align_bytes=64) for g in range(GROUPS)]
        w_codes = [keep.tile([P, GATES * P], U32, name="w_codes%d" % j, align_bytes=64) for j in range(CHUNKS)]
        w_scales = [keep.tile([P, GATES * P], U8, name="w_scales%d" % j, align_bytes=64) for j in range(CHUNKS)]
        grouped_tiles = {}

        def grouped_for(key):
            if key not in grouped_tiles:
                grouped_tiles[key] = work.tile([P, 4 * I], BF16, name="grouped", bufs=4, align_bytes=64)
            return grouped_tiles[key]

        whh_pair = [keep.tile([P, GATES, CHUNKS, P], BF16, name="whh_t%d" % n) for n in range(2)]
        whh_t = [whh_pair[j % 2] for j in range(CHUNKS)]
        base = [keep.tile([P, GATES, P], F32, name="base%d" % j) for j in range(CHUNKS)]
        h0_t = keep.tile([P, CHUNKS, P], BF16, name="h0_t")
        c_last = keep.tile([P, H], F32, name="c_last")

        def copy_on(engine, out, in_):
            if engine == "vector":
                nc.vector.tensor_copy(out=out, in_=in_)
            else:
                nc.scalar.copy(out=out, in_=in_)

        def bank_for(shape, dtype, name, tag):
            return psum.tile(shape, dtype, name=name, tag=tag, bufs=2 if tag == "prep" else 1)

        def turn_words(src, grouped, half, tag):
            words = src[:].rearrange("p q k -> p (q k)").bitcast(F32)
            bank = bank_for([P, 2, 2, P], F32, "bank_words", tag)
            for r in range(2):
                w0 = (2 * half + r) * (I // 2)
                for u in range(2):
                    nc.tensor.transpose(bank[:, r, u, :], words[:, w0 + u:w0 + I // 2:2], ident_f[:])
            dst = grouped[:].bitcast(F32).rearrange("p (q c u) -> p q c u", q=4, u=2)[:, 2 * half:2 * half + 2]
            return lambda engine: copy_on(engine, dst, bank[:].rearrange("p r u c -> p r c u"))

        def turn_x(g, half):
            return turn_words(x_sb[g], grouped_for(("x", g)), half, "prep")

        def turn_wih(j, half, tag="prep"):
            return turn_words(wih_sb[j], grouped_for(("w", j)), half, tag)

        def turn_whh(j, half, tag="prep"):
            bank = bank_for([P, 2, CHUNKS, P], BF16, "bank_whh", tag)
            for r in range(2):
                for kc in range(CHUNKS):
                    nc.tensor.matmul(bank[:, r, kc, :], lhsT=whh_sb[j][:, 2 * half + r, kc * P:(kc + 1) * P], rhs=ident_b[:],
                                     is_transpose=j >= 2, start=True, stop=True)
            return lambda engine: copy_on(engine, whh_t[j][:, 2 * half:2 * half + 2], bank[:])

        def base_gates(j, half, tag="prep"):
            bank = bank_for([P, 2, P], F32, "bank_base", tag)
            for r in range(2):
                gate = 2 * half + r
                bias = bias_rows[:, gate * H + j * P:gate * H + (j + 1) * P]
                pairs = [(whh_t[j][:, gate, kc, :], h0_t[:, kc, :]) for kc in range(CHUNKS)] + [(bias, ones_b[:])]
                for n, (by_channel, by_row) in enumerate(pairs):
                    lhsT, rhs = (by_row, by_channel) if gate == GATE_O else (by_channel, by_row)
                    nc.tensor.matmul(bank[:, r, :], lhsT=lhsT, rhs=rhs, start=(n == 0), stop=(n == len(pairs) - 1))
            return lambda engine: copy_on(engine, base[j][:, 2 * half:2 * half + 2], bank[:])

        def quantize(grouped, codes, scales, lo, hi):
            nc.vector.quantize_mx(out=codes[:, lo * P:hi * P].bitcast(E5M2X4), scales=scales[:, lo * P:hi * P],
                                  in_=grouped[:, lo * I:hi * I])

        def quantize_x(g):
            quantize(grouped_for(("x", g)), x_codes[g], x_scales[g], 0, STEPS)

        def quantize_wih(j, lo=0, hi=GATES):
            quantize(grouped_for(("w", j)), w_codes[j], w_scales[j], lo, hi)

        gate_bank, pre, act, prod_f, prod_i, c_bank, tanh_c, h_raw = {}, {}, {}, {}, {}, {}, {}, {}

        def project(s, gates):
            j, g = order[s]
            for gate in gates:
                bank = bank_for([P, STEPS, P], F32, "bank_gate", "gate%d" % gate)
                cols = slice(gate * P, (gate + 1) * P)
                if gate == GATE_O:
                    for t in range(STEPS):
                        rows = slice(t * P, (t + 1) * P)
                        nc.tensor.matmul_mx(
                            out=bank[:, t, :],
                            lhsT=x_codes[g][:, rows].bitcast(E5M2X4), lhsT_scale=x_scales[g][:, rows],
                            rhs=w_codes[j][:, cols].bitcast(E5M2X4), rhs_scale=w_scales[j][:, cols],
                            start=True, stop=True)
                else:
                    nc.tensor.matmul_mx(
                        out=bank[:].rearrange("p t b -> p (t b)"),
                        lhsT=w_codes[j][:, cols].bitcast(E5M2X4), lhsT_scale=w_scales[j][:, cols],
                        rhs=x_codes[g][:].bitcast(E5M2X4), rhs_scale=x_scales[g][:],
                        start=True, stop=True)
                gate_bank[s, gate] = bank

        def over_steps(ap):
            return ap.unsqueeze(1).to_broadcast([P, STEPS, P])

        def add_base(s, gate):
            j = order[s][0]
            pre[s, gate] = work.tile([P, STEPS, P], F32, name="pre", tag="pre%d" % gate, bufs=2)
            nc.vector.tensor_tensor(out=pre[s, gate][:], in0=over_steps(base[j][:, gate, :]),
                                    in1=gate_bank[s, gate][:], op=ALU.add)

        left, right = {}, {}

        def factor(tiles, name, tick, part):
            if tick not in tiles:
                tiles[tick] = work.tile([P, 2, STEPS, P], F32, name=name, bufs=EMIT_LAG + 1)
            return tiles[tick][:, part]

        def activate(s, gate):
            if gate == GATE_F:
                act[s, gate] = work.tile([P, STEPS, P], F32, name="act_f")[:]
            elif gate == GATE_I:
                act[s, gate] = factor(left, "left", s + 1, 0)
            elif gate == GATE_G:
                act[s, gate] = factor(right, "right", s + 1, 0)
            else:
                act[s, gate] = factor(left, "left", s + EMIT_LAG, 1)
            nc.scalar.activation(out=act[s, gate], in_=pre[s, gate][:],
                                 func=ACT.Tanh if gate == GATE_G else ACT.Sigmoid)

        def gate_step(s, gate):
            add_base(s, gate)
            activate(s, gate)

        def forget(s):
            j = order[s][0]
            prod_f[s] = work.tile([P, STEPS, P], F32, name="prod_f")[:]
            nc.vector.tensor_tensor(out=prod_f[s], in0=act[s, GATE_F], in1=over_steps(consts[:, 0, j, :]), op=ALU.mult)

        def admit(s, engine):
            prod_i[s] = work.tile([P, STEPS, P], F32, name="prod_i", bufs=2)[:]
            engine.tensor_tensor(out=prod_i[s], in0=act[s, GATE_I], in1=act[s, GATE_G], op=ALU.mult)

        def emit(s, engine):
            h_raw[s] = work.tile([P, STEPS, P], F32, name="h_raw")[:]
            engine.tensor_tensor(out=h_raw[s], in0=act[s, GATE_O], in1=tanh_c[s], op=ALU.mult)

        def products(tick):
            both = work.tile([P, 2, STEPS, P], F32, name="both")
            nc.gpsimd.tensor_tensor(out=both[:], in0=left[tick][:], in1=right[tick][:], op=ALU.mult)
            prod_i[tick - 1] = both[:, 0]
            h_raw[tick - EMIT_LAG] = both[:, 1]

        def sum_cell(s, tag="cell"):
            mx_follows = s < last - 1
            c_bank[s] = bank_for([P, STEPS, P], F32, "bank_c", tag)
            for t in range(STEPS):
                nc.tensor.matmul(c_bank[s][:, t, :], lhsT=prod_f[s][:, t, :], rhs=ident_f[:],
                                 is_transpose=not (mx_follows and t == 0), start=True, stop=False)
                nc.tensor.matmul(c_bank[s][:, t, :], lhsT=prod_i[s][:, t, :], rhs=ident_f[:],
                                 is_transpose=not (mx_follows and t == STEPS - 1), start=False, stop=True)

        def squash_cell(s):
            j, g = order[s]
            tanh_c[s] = factor(right, "right", s + EMIT_LAG, 1)
            nc.scalar.activation(out=tanh_c[s], in_=c_bank[s][:], func=ACT.Tanh)
            if g == GROUPS - 1:
                nc.scalar.copy(out=c_last[:, j * P:(j + 1) * P], in_=c_bank[s][:, STEPS - 1, :])

        def add_noise_and_store(s, on_vector):
            j, g = order[s]
            cols = slice(j * P, (j + 1) * P)
            h_out = work.tile([P, STEPS, P], F32, name="h_out", bufs=6)
            if on_vector:
                nc.vector.tensor_tensor(out=h_out[:], in0=h_raw[s], in1=over_steps(consts[:, 1, j, :]), op=ALU.add)
            else:
                nc.gpsimd.tensor_tensor(out=h_out[:], in0=h_raw[s], in1=over_steps(noise_sb[:, cols]), op=ALU.add)
            if g == GROUPS - 1:
                nc.sync.dma_start(out=out_state[1, :, cols], in_=c_last[:, cols])
            nc.sync.dma_start(out=out_h[g * STEPS:(g + 1) * STEPS, :, cols].rearrange("t b c -> b t c"), in_=h_out[:])
            if g == GROUPS - 1:
                nc.sync.dma_start(out=out_state[0, :, cols], in_=h_out[:, STEPS - 1, :])

        turn_x(0, 0)("scalar")
        bank_h0 = bank_for([P, CHUNKS, P], BF16, "bank_h0", "cell")
        for kc in range(CHUNKS):
            nc.tensor.matmul(bank_h0[:, kc, :], lhsT=h0_sb[:, kc * P:(kc + 1) * P], rhs=ident_b[:], start=True, stop=True)
        nc.scalar.copy(out=h0_t[:], in_=bank_h0[:])
        turn_whh(0, 0, "gate2")("vector")
        turn_x(0, 1)("vector")
        turn_wih(0, 0, "gate3")("scalar")
        base_gates(0, 0, "cell")("scalar")
        quantize_x(0)
        quantize_wih(0, 0, 2)
        turn_whh(0, 1, "gate2")("scalar")
        turn_wih(0, 1)("scalar")
        project(0, (GATE_F, GATE_I))

        gate_step(0, GATE_F)
        quantize_wih(0, 2, GATES)
        add_base(0, GATE_I)
        turn_x(1, 0)("vector")
        base_gates(0, 1, "cell")("vector")
        turn_x(1, 1)("vector")
        activate(0, GATE_I)
        project(0, (GATE_G, GATE_O))
        copy_x = turn_x(2, 0)
        copy_whh = turn_whh(1, 0, "cell")
        gate_step(0, GATE_G)
        quantize_x(1)
        copy_x("scalar")
        gate_step(0, GATE_O)
        project(1, (GATE_F, GATE_I))
        turn_x(2, 1)("scalar")
        consts = bank_for([P, 2, CHUNKS, P], BF16, "consts", "consts")
        for j in range(CHUNKS):
            nc.tensor.matmul(consts[:, 0, j, :], lhsT=c0_sb[:, j * P:(j + 1) * P], rhs=ident_b[:], start=True, stop=True)
        nc.tensor.matmul(consts[:, 1].rearrange("p j c -> p (j c)"), lhsT=ident_b[:], rhs=noise_sb[:], start=True, stop=True)
        project(1, (GATE_G, GATE_O))
        admit(0, nc.gpsimd)

        gate_step(1, GATE_F)
        gate_step(1, GATE_I)
        copy_whh("vector")
        copy_whh = turn_whh(1, 1, "cell")
        copy_wih_if = turn_wih(1, 0)
        quantize_x(2)
        project(2, (GATE_F, GATE_I))
        copy_wih_go = turn_wih(1, 1)
        gate_step(1, GATE_G)
        copy_whh("vector")
        forget(0)
        copy_wih_if("scalar")
        copy_wih_go("scalar")
        gate_step(1, GATE_O)
        sum_cell(0)
        copy_base_if = base_gates(1, 0)
        project(2, (GATE_G, GATE_O))
        admit(1, nc.gpsimd)

        copy_base_go = base_gates(1, 1)
        gate_step(2, GATE_F)
        squash_cell(0)
        gate_step(2, GATE_I)
        quantize_wih(1)
        forget(1)
        project(3, (GATE_F, GATE_I))
        copy_base_if("scalar")
        gate_step(2, GATE_G)
        sum_cell(1)
        copy_base_go("scalar")
        copy_x = turn_x(3, 0)
        gate_step(2, GATE_O)
        project(3, (GATE_G, GATE_O))
        copies = [copy_x, turn_x(3, 1)]

        jobs = {s: [] for s in range(UNITS)}
        quantize_at = {}
        for g in range(HEAD_TICKS, GROUPS):
            first = order.index((0, g))
            quantize_at[first - QUANTIZE_LEAD] = (quantize_x, g)
            if g > HEAD_TICKS:
                for half in range(2):
                    jobs[first - INPUT_LEADS[half]].append((turn_x, g, half))
        for j in (2, 3):
            first = order.index((j, 0))
            quantize_at[first - QUANTIZE_LEAD] = (quantize_wih, j)
            for half in range(2):
                jobs[first - WHH_LEADS[half]].append((turn_whh, j, half))
                jobs[first - BASE_LEADS[half]].append((base_gates, j, half))
                jobs[first - WIH_LEADS[half]].append((turn_wih, j, half))

        for s in range(HEAD_TICKS, last):
            noise_on_vector = s % 2 == 0
            if s >= NOISE_LAG and not noise_on_vector:
                add_noise_and_store(s - NOISE_LAG, False)
            products(s)
            gate_step(s, GATE_F)
            if s in quantize_at:
                quantize_operand, n = quantize_at[s]
                quantize_operand(n)
            gate_step(s, GATE_I)
            squash_cell(s - 2)
            project(s + 1, (GATE_F, GATE_I))
            for copy in copies:
                copy("scalar")
            forget(s - 1)
            gate_step(s, GATE_G)
            gate_step(s, GATE_O)
            project(s + 1, (GATE_G, GATE_O))
            if s >= NOISE_LAG and noise_on_vector:
                add_noise_and_store(s - NOISE_LAG, True)
            sum_cell(s - 1)
            copies = [job(n, half) for job, n, half in jobs[s]]

        emit(last - 3, nc.gpsimd)
        admit(last - 1, nc.gpsimd)
        for gate in (GATE_F, GATE_I, GATE_G):
            gate_step(last, gate)
        squash_cell(last - 2)
        forget(last - 1)
        sum_cell(last - 1, "gate0")
        forget(last)
        admit(last, nc.vector)
        sum_cell(last, "gate1")
        emit(last - 2, nc.gpsimd)
        add_base(last, GATE_O)
        add_noise_and_store(last - 4, True)
        add_noise_and_store(last - 3, True)
        squash_cell(last - 1)
        activate(last, GATE_O)
        emit(last - 1, nc.gpsimd)
        add_noise_and_store(last - 2, True)
        squash_cell(last)
        emit(last, nc.vector)
        add_noise_and_store(last - 1, True)
        add_noise_and_store(last, True)
